import numpy as np
import ml_dtypes


def mxq(x, axis, fmt="e4m3"):
    dtype, down = {"e4m3": (ml_dtypes.float8_e4m3fn, 7), "e5m2": (ml_dtypes.float8_e5m2, 14)}[fmt]
    v = np.moveaxis(np.asarray(x, np.float32).astype(ml_dtypes.bfloat16).astype(np.float64), axis, -1)
    blocks = v.reshape(v.shape[:-1] + (-1, 32))
    amax = np.abs(blocks).max(-1, keepdims=True)
    byte = np.maximum(np.where(amax > 0, np.frexp(amax)[1] - 1 + 127, 0) - down, 1)
    scale = np.exp2(byte - 127.0)
    codes = (blocks / scale).astype(np.float32).astype(dtype).astype(np.float64)
    return np.moveaxis((codes * scale).reshape(v.shape), -1, axis)


WIDE = False


def mx_kscale(k):
    if not WIDE:
        return np.ones(k)
    levels = np.array([10, -10, 5, -5, 0])
    if k % 512:
        return np.exp2(np.random.permutation(np.resize(levels, k // 32))).repeat(32)
    a = np.empty((k // 512, 16))
    for p in range(k // 512):
        a[p, :8] = np.random.permutation(np.resize(levels, 8))
        for g in range(8):
            far = levels[np.abs(levels - a[p, g]) >= 10]
            a[p, g + 8] = far[np.random.randint(len(far))]
    return np.exp2(a.ravel()).repeat(32)


BF16 = ml_dtypes.bfloat16


def bf(x):
    return np.asarray(x, np.float32).astype(BF16)


def f64(x):
    return np.asarray(x).astype(np.float64)


B, I, H = 4096, 512, 512
G = 2 * H
EPS = 1e-5


def ln(v):
    mu = v.mean(-1, keepdims=True)
    var = np.square(v - mu).mean(-1, keepdims=True)
    return (v - mu) / np.sqrt(var + EPS)


def sigmoid(v):
    return 1.0 / (1.0 + np.exp(-v))


def setup_inputs():
    s, t = mx_kscale(I), mx_kscale(H)
    return {"x": bf(np.random.standard_normal((B, I)) * s),
            "h": bf(np.random.standard_normal((B, H)) * t),
            "W_irz": bf(np.random.standard_normal((G, I)) / np.sqrt(I) / s),
            "b_irz": bf(np.random.standard_normal(G) * 0.5),
            "W_hrz": bf(np.random.standard_normal((G, H)) / np.sqrt(H) / t),
            "b_hrz": bf(np.random.standard_normal(G) * 0.5)}


def reference(x, h, W_irz, b_irz, W_hrz, b_hrz):
    i_rz = ln((mxq(f64(x), 1, "e4m3") @ mxq(f64(W_irz), 1, "e4m3").T) + f64(b_irz))
    h_rz = ln((mxq(f64(h), 1, "e4m3") @ mxq(f64(W_hrz), 1, "e4m3").T) + f64(b_hrz))
    return sigmoid(i_rz + h_rz)

@@ -1,0 +1,363 @@
+from contextlib import ExitStack
+
+import concourse.mybir as mybir
+from concourse.masks import make_identity
+
+F32 = mybir.dt.float32
+BF16 = mybir.dt.bfloat16
+U32 = mybir.dt.uint32
+U8 = mybir.dt.uint8
+FP8X4 = mybir.dt.float8_e4m3fn_x4
+ALU = mybir.AluOpType
+ACT = mybir.ActivationFunctionType
+
+P = 128
+B = 4096
+K = 512
+N = 1024
+NT = B // P
+EPS = 1e-5
+FLOPS = 2 * 2 * B * K * N
+CHUNKS = [(0, 2), (2, 2), (4, 4), (8, 8), (16, 8), (24, 8)]
+
+LAG = 5
+GP5 = 0
+HEAD = 2
+PEJ = 3
+AB_BUFS = 8
+
+
+def tile_layernormgrucell_pa_t_kernel(tc, x, h, W_irz, b_irz, W_hrz, b_hrz, out):
+    nc = tc.nc
+    with ExitStack() as ctx:
+        const = ctx.enter_context(tc.tile_pool(name="const", bufs=1))
+        wgp = ctx.enter_context(tc.tile_pool(name="wgp", bufs=2))
+        xgp = ctx.enter_context(tc.tile_pool(name="xgp", bufs=3))
+        xcp = ctx.enter_context(tc.tile_pool(name="xcp", bufs=3))
+        abp = ctx.enter_context(tc.tile_pool(name="abp", bufs=AB_BUFS))
+        op = ctx.enter_context(tc.tile_pool(name="op", bufs=4))
+        jp = ctx.enter_context(tc.tile_pool(name="jp", bufs=2))
+        stp = ctx.enter_context(tc.tile_pool(name="stp", bufs=AB_BUFS + 2))
+        dgp = ctx.enter_context(tc.tile_pool(name="dgp", bufs=2))
+        psp = ctx.enter_context(tc.psum_pool(name="psp", bufs=8))
+        ctx.enter_context(tc.manual_schedule())
+
+        def bank():
+            return psp.tile([P, 512], F32, tag="bank", name="bank")
+
+        ident = const.tile([P, P], F32, name="ident")
+        make_identity(nc, ident[:])
+        brow = const.tile([P, 2 * N], BF16, name="brow")
+        nc.vector.memset(brow[:].bitcast(mybir.dt.int32), 0)
+        ones = const.tile([P, P], BF16, name="ones")
+        nc.vector.memset(ones[:], 1.0)
+        mhalf = const.tile([P, 4], F32, name="mhalf")
+        nc.vector.memset(mhalf[:], -0.5)
+        warm = const.tile([P, 1], F32, name="warm")
+        nc.scalar.activation(out=warm[:], in_=mhalf[:, 0:1], func=ACT.Sigmoid)
+
+        acts = (x, h)
+        wts = (W_irz, W_hrz)
+        xch = [[None] * len(CHUNKS), [None] * len(CHUNKS)]
+        wraw = [[None, None], [None, None]]
+
+        def load_act(o, ci):
+            t0, nt = CHUNKS[ci]
+            t_ = const.tile([P, nt * K], BF16, name="act%d_%d" % (o, ci))
+            nc.sync.dma_start(
+                out=t_[:].rearrange("p (t k) -> p t k", k=K),
+                in_=acts[o].rearrange("(p t) k -> p t k", t=NT)[:, t0 : t0 + nt, :],
+            )
+            xch[o][ci] = t_
+
+        def load_w(o, hf):
+            t_ = const.tile([P, 4 * K], BF16, name="wraw%d_%d" % (o, hf))
+            nc.sync.dma_start(
+                out=t_[:].rearrange("p (j k) -> p j k", k=K),
+                in_=wts[o][hf * 512 : (hf + 1) * 512, :].rearrange("(j p) k -> p j k", p=P),
+            )
+            wraw[o][hf] = t_
+
+        load_w(0, 0)
+        load_act(0, 0)
+        load_act(1, 0)
+        nc.sync.dma_start(out=brow[0:1, 0:N], in_=b_irz.rearrange("(o n) -> o n", o=1))
+        nc.sync.dma_start(out=brow[0:1, N : 2 * N], in_=b_hrz.rearrange("(o n) -> o n", o=1))
+        load_w(0, 1)
+        load_w(1, 0)
+        load_w(1, 1)
+        for ci in range(1, len(CHUNKS)):
+            load_act(0, ci)
+            load_act(1, ci)
+
+        bias = const.tile([P, 2 * N], F32, name="bias")
+
+        def spread_bias():
+            for q in range(4):
+                ps = bank()
+                nc.tensor.matmul(out=ps[:], lhsT=ones[:], rhs=brow[:, q * 512 : (q + 1) * 512], start=True, stop=True)
+                if q % 2 == 0:
+                    nc.vector.tensor_copy(out=bias[:, q * 512 : (q + 1) * 512], in_=ps[:])
+                else:
+                    nc.scalar.copy(out=bias[:, q * 512 : (q + 1) * 512], in_=ps[:])
+
+        wc = [const.tile([P, N], U32, name="wc%d" % o, align_bytes=64) for o in range(2)]
+        wsc = [const.tile([P, N], U8, name="wsc%d" % o, align_bytes=64) for o in range(2)]
+        wgs = {}
+
+        def w_transpose(o, hf, second_on_vector):
+            raw_w = wraw[o][hf][:].bitcast(F32)
+            wg = wgp.tile([P, 2048], BF16, tag="wg", name="wg", align_bytes=64)
+            wg_w = wg[:].bitcast(F32)
+            for pr in range(2):
+                tp = bank()
+                for q in range(4):
+                    c0 = pr * 512 + (q // 2) * 256
+                    nc.tensor.transpose(tp[:, q * P : (q + 1) * P], raw_w[:, c0 + q % 2 : c0 + 256 : 2], ident[:])
+                dst = wg_w[:, pr * 512 : (pr + 1) * 512].rearrange("p (a r u) -> p a r u", a=2, u=2)
+                src = tp[:].rearrange("p (a u r) -> p a r u", a=2, u=2)
+                if pr == 1 and second_on_vector:
+                    nc.vector.tensor_copy(out=dst, in_=src)
+                else:
+                    nc.scalar.copy(out=dst, in_=src)
+            wgs[(o, hf)] = wg
+
+        def w_quantise(o, hf):
+            cols = slice(hf * 512, (hf + 1) * 512)
+            nc.vector.quantize_mx(out=wc[o][:, cols].bitcast(FP8X4), scales=wsc[o][:, cols], in_=wgs[(o, hf)][:])
+
+        def act_words(o, t):
+            for ci in range(len(CHUNKS)):
+                t0, nt = CHUNKS[ci]
+                if t0 <= t < t0 + nt:
+                    return xch[o][ci][:].bitcast(F32)[:, (t - t0) * 256 : (t - t0 + 1) * 256]
+            raise ValueError("no chunk")
+
+        dgs = {}
+        tps = {}
+        xgs = {}
+        xcs = {}
+        pss = {}
+        abs_ = {}
+        sts = {}
+
+        def ok(t):
+            return 0 <= t < NT
+
+        def on_gpsimd(t):
+            return GP5 > 0 and t % GP5 == GP5 - 1 and t < NT - 4
+
+        def s_tr(t):
+            tp = bank()
+            for o in range(2):
+                w_ = act_words(o, t)
+                for u in range(2):
+                    q = 2 * o + u
+                    nc.tensor.transpose(tp[:, q * P : (q + 1) * P], w_[:, u : 256 : 2], ident[:])
+            tps[t] = tp
+
+        def s_ev(t):
+            xg = xgp.tile([P, 1024], BF16, tag="xg", name="xg", align_bytes=64)
+            dst = xg[:].bitcast(F32).rearrange("p (a r u) -> p a r u", a=2, u=2)
+            src = tps[t][:].rearrange("p (a u r) -> p a r u", a=2, u=2)
+            if (t % 3 == 0) and t >= 4:
+                nc.vector.tensor_copy(out=dst, in_=src)
+            else:
+                nc.scalar.copy(out=dst, in_=src)
+            xgs[t] = xg
+
+        def s_q(t):
+            xc = xcp.tile([P, 256], U32, tag="xc", name="xc", align_bytes=64)
+            xs = xcp.tile([P, 256], U8, tag="xs", name="xs", align_bytes=64)
+            nc.vector.quantize_mx(out=xc[:].bitcast(FP8X4), scales=xs[:], in_=xgs[t][:])
+            xcs[t] = (xc, xs)
+
+        def s_mx(t, o, hf):
+            xc, xs = xcs[t]
+            cols = slice(hf * 512, (hf + 1) * 512)
+            ps = bank()
+            nc.tensor.matmul_mx(
+                out=ps[:],
+                lhsT=xc[:, o * P : (o + 1) * P].bitcast(FP8X4),
+                lhsT_scale=xs[:, o * P : (o + 1) * P],
+                rhs=wc[o][:, cols].bitcast(FP8X4),
+                rhs_scale=wsc[o][:, cols],
+                start=True,
+                stop=True,
+            )
+            pss[(t, o, hf)] = ps
+
+        def s_p1(t, o, hf):
+            if (o, hf) == (0, 0):
+                abs_[t] = abp.tile([P, 2, N], F32, tag="ab", name="ab")
+                if t % 2 == 0:
+                    sts[t // 2] = {
+                        "sv": stp.tile([P, 2, 4], F32, tag="sv", name="sv"),
+                        "ss": stp.tile([P, 4], F32, tag="ss", name="ss"),
+                    }
+            i = (t % 2) * 2 + o
+            nc.vector.scalar_tensor_tensor(
+                out=abs_[t][:, o, hf * 512 : (hf + 1) * 512],
+                in0=pss[(t, o, hf)][:],
+                scalar=-1.0,
+                in1=bias[:, o * N + hf * 512 : o * N + (hf + 1) * 512],
+                op0=ALU.mult,
+                op1=ALU.subtract,
+                accum_out=sts[t // 2]["sv"][:, hf, i : i + 1],
+            )
+
+        def s_sq(t, o):
+            i = (t % 2) * 2 + o
+            junk = jp.tile([P, N], BF16, tag="junk", name="junk")
+            nc.scalar.activation(
+                out=junk[:],
+                in_=abs_[t][:, o, :],
+                func=ACT.Square,
+                bias=sts[t // 2]["sv"][:, 0, i : i + 1],
+                scale=-512.0,
+                accum_out=sts[t // 2]["ss"][:, i : i + 1],
+            )
+
+        def small(name, width):
+            return stp.tile([P, width], F32, tag=name, name=name)
+
+        def s_ch(m_):
+            st = sts[m_]
+            s0 = st["sv"][:, 0, :]
+            s1 = st["sv"][:, 1, :]
+            tt = nc.gpsimd.tensor_tensor
+            dd = small("dd", 4)
+            tt(out=dd[:], in0=s1, in1=s0, op=ALU.subtract)
+            d2 = small("d2", 4)
+            tt(out=d2[:], in0=dd[:], in1=dd[:], op=ALU.mult)
+            sm = small("sm", 4)
+            tt(out=sm[:], in0=s0, in1=s1, op=ALU.add)
+            qq = small("qq", 4)
+            nc.gpsimd.tensor_scalar(
+                out=qq[:], in0=st["ss"][:], scalar1=1.0 / 256.0, scalar2=EPS * N * N, op0=ALU.mult, op1=ALU.add
+            )
+            vn = small("vn", 4)
+            tt(out=vn[:], in0=qq[:], in1=d2[:], op=ALU.subtract)
+            rsn = small("rsn", 4)
+            tt(out=rsn[:], in0=vn[:], in1=mhalf[:], op=ALU.pow)
+            vn_v = vn[:].rearrange("p (t o) -> p t o", o=2)
+            rsn_v = rsn[:].rearrange("p (t o) -> p t o", o=2)
+            sdn = small("sdn", 2)
+            tt(out=sdn[:], in0=vn_v[:, :, 1], in1=rsn_v[:, :, 1], op=ALU.mult)
+            rho = small("rho", 2)
+            tt(out=rho[:], in0=sdn[:], in1=rsn_v[:, :, 0], op=ALU.mult)
+            mm_ = small("mm_", 4)
+            tt(out=mm_[:], in0=sm[:], in1=rsn[:], op=ALU.mult)
+            mm_v = mm_[:].rearrange("p (t o) -> p t o", o=2)
+            c = small("c", 2)
+            tt(out=c[:], in0=mm_v[:, :, 0], in1=mm_v[:, :, 1], op=ALU.add)
+            nsc = small("nsc", 2)
+            nc.gpsimd.tensor_scalar(
+                out=nsc[:], in0=rsn_v[:, :, 1], scalar1=-1.0 * N, scalar2=0.0, op0=ALU.mult, op1=ALU.add
+            )
+            st["rho"] = rho
+            st["c"] = c
+            st["nsc"] = nsc
+
+        def on_tensor(t):
+            return PEJ > 0 and t % PEJ == PEJ - 1
+
+        def s_diag(t):
+            dg = dgp.tile([P, P], F32, tag="dg", name="dg")
+            nc.gpsimd.tensor_scalar(
+                out=dg[:], in0=ident[:], scalar1=sts[t // 2]["rho"][:, t % 2 : t % 2 + 1], scalar2=0.0, op0=ALU.mult, op1=ALU.add
+            )
+            dgs[t] = dg
+
+        def s_join_pe(t):
+            ab = abs_[t]
+            for hf in range(2):
+                cols = slice(hf * 512, (hf + 1) * 512)
+                ps = bank()
+                nc.tensor.matmul(out=ps[:], lhsT=dgs[t][:], rhs=ab[:, 0, cols], start=True, stop=False)
+                nc.tensor.matmul(out=ps[:], lhsT=ident[:], rhs=ab[:, 1, cols], start=False, stop=True)
+                pss[("j", t, hf)] = ps
+
+        def s_p5(t):
+            ab = abs_[t]
+            rho = sts[t // 2]["rho"][:, t % 2 : t % 2 + 1]
+            if on_gpsimd(t):
+                nc.gpsimd.tensor_scalar(out=ab[:, 0, :], in0=ab[:, 0, :], scalar1=rho, scalar2=0.0, op0=ALU.mult, op1=ALU.add)
+                nc.gpsimd.tensor_tensor(out=ab[:, 1, :], in0=ab[:, 0, :], in1=ab[:, 1, :], op=ALU.add)
+            else:
+                nc.vector.scalar_tensor_tensor(
+                    out=ab[:, 1, :], in0=ab[:, 0, :], scalar=rho, in1=ab[:, 1, :], op0=ALU.mult, op1=ALU.add
+                )
+
+        def s_sig(t):
+            ot = op.tile([P, N], F32, tag="ot", name="ot")
+            c_ = sts[t // 2]["c"][:, t % 2 : t % 2 + 1]
+            nsc_ = sts[t // 2]["nsc"][:, t % 2 : t % 2 + 1]
+            if on_tensor(t):
+                for hf in range(2):
+                    nc.scalar.activation(
+                        out=ot[:, hf * 512 : (hf + 1) * 512], in_=pss[("j", t, hf)][:], func=ACT.Sigmoid, bias=c_, scale=nsc_
+                    )
+            else:
+                nc.scalar.activation(out=ot[:], in_=abs_[t][:, 1, :], func=ACT.Sigmoid, bias=c_, scale=nsc_)
+            nc.sync.dma_start(out=out.rearrange("(p t) j -> p t j", t=NT)[:, t, :], in_=ot[:])
+
+        w_transpose(0, 0, True)
+        w_quantise(0, 0)
+        for t in range(HEAD):
+            s_tr(t)
+            s_ev(t)
+            s_q(t)
+        spread_bias()
+        w_transpose(0, 1, False)
+        for (o, hf) in ((0, 0), (0, 1), (1, 0), (1, 1)):
+            for t in range(HEAD):
+                s_mx(t, o, hf)
+            for t in range(HEAD):
+                s_p1(t, o, hf)
+            if (o, hf) == (0, 0):
+                w_quantise(0, 1)
+                w_transpose(1, 0, False)
+            if (o, hf) == (0, 1):
+                w_quantise(1, 0)
+                w_transpose(1, 1, False)
+            if (o, hf) == (1, 0):
+                w_quantise(1, 1)
+                for t in range(HEAD):
+                    s_sq(t, 0)
+                for t in (2, 3):
+                    s_tr(t)
+                    s_ev(t)
+        s_q(2)
+        s_tr(4)
+
+        for it in range(NT + LAG):
+            if ok(it + 2) and it + 2 > HEAD:
+                s_q(it + 2)
+            if ok(it) and it >= HEAD:
+                for o in range(2):
+                    for hf in range(2):
+                        s_p1(it, o, hf)
+            if ok(it + 1) and it + 1 >= HEAD:
+                for o in range(2):
+                    for hf in range(2):
+                        s_mx(it + 1, o, hf)
+            if ok(it + 5):
+                s_tr(it + 5)
+            if it % 2 == 0 and ok(it - 2):
+                s_ch((it - 2) // 2)
+                for t in (it - 2, it - 1):
+                    if on_tensor(t):
+                        s_diag(t)
+            if ok(it - LAG + 1) and on_tensor(it - LAG + 1):
+                s_join_pe(it - LAG + 1)
+            if ok(it - LAG) and not on_tensor(it - LAG):
+                s_p5(it - LAG)
+            if ok(it):
+                if it >= HEAD:
+                    s_sq(it, 0)
+                s_sq(it, 1)
+            if ok(it - LAG):
+                s_sig(it - LAG)
+            if ok(it + 4):
+                s_ev(it + 4)

@@ -21,9 +21,12 @@ FLOPS = 2 * 2 * B * K * N
 CHUNKS = [(0, 2), (2, 2), (4, 4), (8, 8), (16, 8), (24, 8)]
 
 LAG = 5
-GP5 = 0
 HEAD = 2
-PEJ = 3
+JOIN = "VVP"
+GW = 256
+EVV = "-"
+EVT = 32
+QB = 1
 AB_BUFS = 8
 
 
@@ -38,12 +41,12 @@ def tile_layernormgrucell_pa_t_kernel(tc, x, h, W_irz, b_irz, W_hrz, b_hrz, out)
         op = ctx.enter_context(tc.tile_pool(name="op", bufs=4))
         jp = ctx.enter_context(tc.tile_pool(name="jp", bufs=2))
         stp = ctx.enter_context(tc.tile_pool(name="stp", bufs=AB_BUFS + 2))
-        dgp = ctx.enter_context(tc.tile_pool(name="dgp", bufs=2))
+        dgp = ctx.enter_context(tc.tile_pool(name="dgp", bufs=3))
         psp = ctx.enter_context(tc.psum_pool(name="psp", bufs=8))
         ctx.enter_context(tc.manual_schedule())
 
-        def bank():
-            return psp.tile([P, 512], F32, tag="bank", name="bank")
+        def bank(dt=F32, width=512):
+            return psp.tile([P, width], dt, tag="bank", name="bank")
 
         ident = const.tile([P, P], F32, name="ident")
         make_identity(nc, ident[:])
@@ -90,16 +93,20 @@ def tile_layernormgrucell_pa_t_kernel(tc, x, h, W_irz, b_irz, W_hrz, b_hrz, out)
             load_act(0, ci)
             load_act(1, ci)
 
-        bias = const.tile([P, 2 * N], F32, name="bias")
+        bias = const.tile([P, 2 * N], BF16, name="bias")
 
         def spread_bias():
-            for q in range(4):
-                ps = bank()
-                nc.tensor.matmul(out=ps[:], lhsT=ones[:], rhs=brow[:, q * 512 : (q + 1) * 512], start=True, stop=True)
-                if q % 2 == 0:
-                    nc.vector.tensor_copy(out=bias[:, q * 512 : (q + 1) * 512], in_=ps[:])
+            for o in range(2):
+                ps = bank(BF16, N)
+                for hf in range(2):
+                    c0 = hf * 512
+                    nc.tensor.matmul(
+                        out=ps[:, c0 : c0 + 512], lhsT=ones[:], rhs=brow[:, o * N + c0 : o * N + c0 + 512], start=True, stop=True
+                    )
+                if o == 0:
+                    nc.vector.tensor_copy(out=bias[:, 0:N], in_=ps[:])
                 else:
-                    nc.scalar.copy(out=bias[:, q * 512 : (q + 1) * 512], in_=ps[:])
+                    nc.scalar.copy(out=bias[:, N : 2 * N], in_=ps[:])
 
         wc = [const.tile([P, N], U32, name="wc%d" % o, align_bytes=64) for o in range(2)]
         wsc = [const.tile([P, N], U8, name="wsc%d" % o, align_bytes=64) for o in range(2)]
@@ -144,8 +151,8 @@ def tile_layernormgrucell_pa_t_kernel(tc, x, h, W_irz, b_irz, W_hrz, b_hrz, out)
         def ok(t):
             return 0 <= t < NT
 
-        def on_gpsimd(t):
-            return GP5 > 0 and t % GP5 == GP5 - 1 and t < NT - 4
+        def kind(t):
+            return JOIN[t % len(JOIN)]
 
         def s_tr(t):
             tp = bank()
@@ -153,33 +160,37 @@ def tile_layernormgrucell_pa_t_kernel(tc, x, h, W_irz, b_irz, W_hrz, b_hrz, out)
                 w_ = act_words(o, t)
                 for u in range(2):
                     q = 2 * o + u
-                    nc.tensor.transpose(tp[:, q * P : (q + 1) * P], w_[:, u : 256 : 2], ident[:])
+                    nc.tensor.transpose(tp[:, q * P : (q + 1) * P], w_[:, u:256:2], ident[:])
             tps[t] = tp
 
         def s_ev(t):
-            xg = xgp.tile([P, 1024], BF16, tag="xg", name="xg", align_bytes=64)
-            dst = xg[:].bitcast(F32).rearrange("p (a r u) -> p a r u", a=2, u=2)
+            if t % QB == 0:
+                xg = xgp.tile([P, QB * 1024], BF16, tag="xg", name="xg", align_bytes=64)
+                xgs[t // QB] = xg
+            s = (t % QB) * 512
+            dst = xgs[t // QB][:].bitcast(F32)[:, s : s + 512].rearrange("p (a r u) -> p a r u", a=2, u=2)
             src = tps[t][:].rearrange("p (a u r) -> p a r u", a=2, u=2)
-            if (t % 3 == 0) and t >= 4:
+            if (EVV[t % len(EVV)] == "V" or t >= EVT) and t >= 4:
                 nc.vector.tensor_copy(out=dst, in_=src)
             else:
                 nc.scalar.copy(out=dst, in_=src)
-            xgs[t] = xg
 
         def s_q(t):
-            xc = xcp.tile([P, 256], U32, tag="xc", name="xc", align_bytes=64)
-            xs = xcp.tile([P, 256], U8, tag="xs", name="xs", align_bytes=64)
-            nc.vector.quantize_mx(out=xc[:].bitcast(FP8X4), scales=xs[:], in_=xgs[t][:])
-            xcs[t] = (xc, xs)
+            if t % QB == 0:
+                xc = xcp.tile([P, QB * 256], U32, tag="xc", name="xc", align_bytes=64)
+                xs = xcp.tile([P, QB * 256], U8, tag="xs", name="xs", align_bytes=64)
+                nc.vector.quantize_mx(out=xc[:].bitcast(FP8X4), scales=xs[:], in_=xgs[t // QB][:])
+                xcs[t // QB] = (xc, xs)
 
         def s_mx(t, o, hf):
-            xc, xs = xcs[t]
+            xc, xs = xcs[t // QB]
             cols = slice(hf * 512, (hf + 1) * 512)
+            c0 = (t % QB) * 256 + o * P
             ps = bank()
             nc.tensor.matmul_mx(
                 out=ps[:],
-                lhsT=xc[:, o * P : (o + 1) * P].bitcast(FP8X4),
-                lhsT_scale=xs[:, o * P : (o + 1) * P],
+                lhsT=xc[:, c0 : c0 + P].bitcast(FP8X4),
+                lhsT_scale=xs[:, c0 : c0 + P],
                 rhs=wc[o][:, cols].bitcast(FP8X4),
                 rhs_scale=wsc[o][:, cols],
                 start=True,
@@ -259,9 +270,6 @@ def tile_layernormgrucell_pa_t_kernel(tc, x, h, W_irz, b_irz, W_hrz, b_hrz, out)
             st["c"] = c
             st["nsc"] = nsc
 
-        def on_tensor(t):
-            return PEJ > 0 and t % PEJ == PEJ - 1
-
         def s_diag(t):
             dg = dgp.tile([P, P], F32, tag="dg", name="dg")
             nc.gpsimd.tensor_scalar(
@@ -269,31 +277,34 @@ def tile_layernormgrucell_pa_t_kernel(tc, x, h, W_irz, b_irz, W_hrz, b_hrz, out)
             )
             dgs[t] = dg
 
-        def s_join_pe(t):
+        def s_join_pe(t, hf):
             ab = abs_[t]
-            for hf in range(2):
-                cols = slice(hf * 512, (hf + 1) * 512)
-                ps = bank()
-                nc.tensor.matmul(out=ps[:], lhsT=dgs[t][:], rhs=ab[:, 0, cols], start=True, stop=False)
-                nc.tensor.matmul(out=ps[:], lhsT=ident[:], rhs=ab[:, 1, cols], start=False, stop=True)
-                pss[("j", t, hf)] = ps
+            cols = slice(hf * 512, (hf + 1) * 512)
+            ps = bank()
+            nc.tensor.matmul(out=ps[:], lhsT=dgs[t][:], rhs=ab[:, 0, cols], start=True, stop=False)
+            nc.tensor.matmul(out=ps[:], lhsT=ident[:], rhs=ab[:, 1, cols], start=False, stop=True)
+            pss[("j", t, hf)] = ps
 
-        def s_p5(t):
+        def s_join_g(t):
             ab = abs_[t]
             rho = sts[t // 2]["rho"][:, t % 2 : t % 2 + 1]
-            if on_gpsimd(t):
-                nc.gpsimd.tensor_scalar(out=ab[:, 0, :], in0=ab[:, 0, :], scalar1=rho, scalar2=0.0, op0=ALU.mult, op1=ALU.add)
-                nc.gpsimd.tensor_tensor(out=ab[:, 1, :], in0=ab[:, 0, :], in1=ab[:, 1, :], op=ALU.add)
-            else:
-                nc.vector.scalar_tensor_tensor(
-                    out=ab[:, 1, :], in0=ab[:, 0, :], scalar=rho, in1=ab[:, 1, :], op0=ALU.mult, op1=ALU.add
-                )
+            for c0 in range(0, N, GW):
+                cols = slice(c0, c0 + GW)
+                nc.gpsimd.tensor_scalar(out=ab[:, 0, cols], in0=ab[:, 0, cols], scalar1=rho, scalar2=0.0, op0=ALU.mult, op1=ALU.add)
+                nc.gpsimd.tensor_tensor(out=ab[:, 1, cols], in0=ab[:, 0, cols], in1=ab[:, 1, cols], op=ALU.add)
+
+        def s_join_v(t):
+            ab = abs_[t]
+            rho = sts[t // 2]["rho"][:, t % 2 : t % 2 + 1]
+            nc.vector.scalar_tensor_tensor(
+                out=ab[:, 1, :], in0=ab[:, 0, :], scalar=rho, in1=ab[:, 1, :], op0=ALU.mult, op1=ALU.add
+            )
 
         def s_sig(t):
             ot = op.tile([P, N], F32, tag="ot", name="ot")
             c_ = sts[t // 2]["c"][:, t % 2 : t % 2 + 1]
             nsc_ = sts[t // 2]["nsc"][:, t % 2 : t % 2 + 1]
-            if on_tensor(t):
+            if kind(t) == "P":
                 for hf in range(2):
                     nc.scalar.activation(
                         out=ot[:, hf * 512 : (hf + 1) * 512], in_=pss[("j", t, hf)][:], func=ACT.Sigmoid, bias=c_, scale=nsc_
@@ -308,6 +319,8 @@ def tile_layernormgrucell_pa_t_kernel(tc, x, h, W_irz, b_irz, W_hrz, b_hrz, out)
             s_tr(t)
             s_ev(t)
             s_q(t)
+        if QB == 2:
+            s_q(0)
         spread_bias()
         w_transpose(0, 1, False)
         for (o, hf) in ((0, 0), (0, 1), (1, 0), (1, 1)):
@@ -347,12 +360,18 @@ def tile_layernormgrucell_pa_t_kernel(tc, x, h, W_irz, b_irz, W_hrz, b_hrz, out)
             if it % 2 == 0 and ok(it - 2):
                 s_ch((it - 2) // 2)
                 for t in (it - 2, it - 1):
-                    if on_tensor(t):
+                    if kind(t) == "P":
                         s_diag(t)
-            if ok(it - LAG + 1) and on_tensor(it - LAG + 1):
-                s_join_pe(it - LAG + 1)
-            if ok(it - LAG) and not on_tensor(it - LAG):
-                s_p5(it - LAG)
+            t = it - LAG + 1
+            if ok(t) and kind(t) == "P":
+                for hf in range(2):
+                    s_join_pe(t, hf)
+            t = it - LAG + 2
+            if ok(t) and kind(t) == "G":
+                s_join_g(t)
+            t = it - LAG
+            if ok(t) and kind(t) == "V":
+                s_join_v(t)
             if ok(it):
                 if it >= HEAD:
                     s_sq(it, 0)

@@ -20,14 +20,17 @@ EPS = 1e-5
 FLOPS = 2 * 2 * B * K * N
 CHUNKS = [(0, 2), (2, 2), (4, 4), (8, 8), (16, 8), (24, 8)]
 
-LAG = 5
+LAG = 7
 HEAD = 2
 JOIN = "VVP"
-GW = 256
+GROUPS = [4] * 7 + [2, 2]
+PJ = 1
+POWW = 8
+CHD = 1
 EVV = "-"
 EVT = 32
 QB = 1
-AB_BUFS = 8
+AB_BUFS = 10
 
 
 def tile_layernormgrucell_pa_t_kernel(tc, x, h, W_irz, b_irz, W_hrz, b_hrz, out):
@@ -54,7 +57,7 @@ def tile_layernormgrucell_pa_t_kernel(tc, x, h, W_irz, b_irz, W_hrz, b_hrz, out)
         nc.vector.memset(brow[:].bitcast(mybir.dt.int32), 0)
         ones = const.tile([P, P], BF16, name="ones")
         nc.vector.memset(ones[:], 1.0)
-        mhalf = const.tile([P, 4], F32, name="mhalf")
+        mhalf = const.tile([P, 8], F32, name="mhalf")
         nc.vector.memset(mhalf[:], -0.5)
         warm = const.tile([P, 1], F32, name="warm")
         nc.scalar.activation(out=warm[:], in_=mhalf[:, 0:1], func=ACT.Sigmoid)
@@ -148,6 +151,15 @@ def tile_layernormgrucell_pa_t_kernel(tc, x, h, W_irz, b_irz, W_hrz, b_hrz, out)
         abs_ = {}
         sts = {}
 
+        gsize = {}
+        gstart = {}
+        t0_ = 0
+        for g_ in GROUPS:
+            gsize[t0_] = g_
+            for t in range(t0_, t0_ + g_):
+                gstart[t] = t0_
+            t0_ += g_
+
         def ok(t):
             return 0 <= t < NT
 
@@ -201,12 +213,12 @@ def tile_layernormgrucell_pa_t_kernel(tc, x, h, W_irz, b_irz, W_hrz, b_hrz, out)
         def s_p1(t, o, hf):
             if (o, hf) == (0, 0):
                 abs_[t] = abp.tile([P, 2, N], F32, tag="ab", name="ab")
-                if t % 2 == 0:
-                    sts[t // 2] = {
-                        "sv": stp.tile([P, 2, 4], F32, tag="sv", name="sv"),
-                        "ss": stp.tile([P, 4], F32, tag="ss", name="ss"),
+                if t in gsize:
+                    sts[t] = {
+                        "sv": stp.tile([P, 2, 8], F32, tag="sv", name="sv"),
+                        "ss": stp.tile([P, 8], F32, tag="ss", name="ss"),
                     }
-            i = (t % 2) * 2 + o
+            i = (t - gstart[t]) * 2 + o
             nc.vector.scalar_tensor_tensor(
                 out=abs_[t][:, o, hf * 512 : (hf + 1) * 512],
                 in0=pss[(t, o, hf)][:],
@@ -214,57 +226,61 @@ def tile_layernormgrucell_pa_t_kernel(tc, x, h, W_irz, b_irz, W_hrz, b_hrz, out)
                 in1=bias[:, o * N + hf * 512 : o * N + (hf + 1) * 512],
                 op0=ALU.mult,
                 op1=ALU.subtract,
-                accum_out=sts[t // 2]["sv"][:, hf, i : i + 1],
+                accum_out=sts[gstart[t]]["sv"][:, hf, i : i + 1],
             )
 
         def s_sq(t, o):
-            i = (t % 2) * 2 + o
+            i = (t - gstart[t]) * 2 + o
             junk = jp.tile([P, N], BF16, tag="junk", name="junk")
             nc.scalar.activation(
                 out=junk[:],
                 in_=abs_[t][:, o, :],
                 func=ACT.Square,
-                bias=sts[t // 2]["sv"][:, 0, i : i + 1],
+                bias=sts[gstart[t]]["sv"][:, 0, i : i + 1],
                 scale=-512.0,
-                accum_out=sts[t // 2]["ss"][:, i : i + 1],
+                accum_out=sts[gstart[t]]["ss"][:, i : i + 1],
             )
 
         def small(name, width):
-            return stp.tile([P, width], F32, tag=name, name=name)
+            t_ = stp.tile([P, 8], F32, tag=name, name=name)
+            return t_[:, 0:width]
 
-        def s_ch(m_):
-            st = sts[m_]
-            s0 = st["sv"][:, 0, :]
-            s1 = st["sv"][:, 1, :]
+        def s_ch(t0):
+            g = gsize[t0]
+            st = sts[t0]
+            s0 = st["sv"][:, 0, 0 : 2 * g]
+            s1 = st["sv"][:, 1, 0 : 2 * g]
             tt = nc.gpsimd.tensor_tensor
-            dd = small("dd", 4)
-            tt(out=dd[:], in0=s1, in1=s0, op=ALU.subtract)
-            d2 = small("d2", 4)
-            tt(out=d2[:], in0=dd[:], in1=dd[:], op=ALU.mult)
-            sm = small("sm", 4)
-            tt(out=sm[:], in0=s0, in1=s1, op=ALU.add)
-            qq = small("qq", 4)
+            dd = small("dd", 2 * g)
+            tt(out=dd[:, :], in0=s1, in1=s0, op=ALU.subtract)
+            d2 = small("d2", 2 * g)
+            tt(out=d2[:, :], in0=dd[:, :], in1=dd[:, :], op=ALU.mult)
+            sm = small("sm", 2 * g)
+            tt(out=sm[:, :], in0=s0, in1=s1, op=ALU.add)
+            qq = small("qq", 2 * g)
             nc.gpsimd.tensor_scalar(
-                out=qq[:], in0=st["ss"][:], scalar1=1.0 / 256.0, scalar2=EPS * N * N, op0=ALU.mult, op1=ALU.add
+                out=qq[:, :], in0=st["ss"][:, 0 : 2 * g], scalar1=1.0 / 256.0, scalar2=EPS * N * N, op0=ALU.mult, op1=ALU.add
             )
-            vn = small("vn", 4)
-            tt(out=vn[:], in0=qq[:], in1=d2[:], op=ALU.subtract)
-            rsn = small("rsn", 4)
-            tt(out=rsn[:], in0=vn[:], in1=mhalf[:], op=ALU.pow)
-            vn_v = vn[:].rearrange("p (t o) -> p t o", o=2)
-            rsn_v = rsn[:].rearrange("p (t o) -> p t o", o=2)
-            sdn = small("sdn", 2)
-            tt(out=sdn[:], in0=vn_v[:, :, 1], in1=rsn_v[:, :, 1], op=ALU.mult)
-            rho = small("rho", 2)
-            tt(out=rho[:], in0=sdn[:], in1=rsn_v[:, :, 0], op=ALU.mult)
-            mm_ = small("mm_", 4)
-            tt(out=mm_[:], in0=sm[:], in1=rsn[:], op=ALU.mult)
-            mm_v = mm_[:].rearrange("p (t o) -> p t o", o=2)
-            c = small("c", 2)
-            tt(out=c[:], in0=mm_v[:, :, 0], in1=mm_v[:, :, 1], op=ALU.add)
-            nsc = small("nsc", 2)
+            vn = small("vn", 2 * g)
+            tt(out=vn[:, :], in0=qq[:, :], in1=d2[:, :], op=ALU.subtract)
+            rsn = small("rsn", 2 * g)
+            for c0 in range(0, 2 * g, POWW):
+                c1 = min(c0 + POWW, 2 * g)
+                tt(out=rsn[:, c0:c1], in0=vn[:, c0:c1], in1=mhalf[:, 0 : c1 - c0], op=ALU.pow)
+            vn_v = vn[:, :].rearrange("p (t o) -> p t o", o=2)
+            rsn_v = rsn[:, :].rearrange("p (t o) -> p t o", o=2)
+            sdn = small("sdn", g)
+            tt(out=sdn[:, :], in0=vn_v[:, :, 1], in1=rsn_v[:, :, 1], op=ALU.mult)
+            rho = small("rho", g)
+            tt(out=rho[:, :], in0=sdn[:, :], in1=rsn_v[:, :, 0], op=ALU.mult)
+            mm_ = small("mm_", 2 * g)
+            tt(out=mm_[:, :], in0=sm[:, :], in1=rsn[:, :], op=ALU.mult)
+            mm_v = mm_[:, :].rearrange("p (t o) -> p t o", o=2)
+            c = small("c", g)
+            tt(out=c[:, :], in0=mm_v[:, :, 0], in1=mm_v[:, :, 1], op=ALU.add)
+            nsc = small("nsc", g)
             nc.gpsimd.tensor_scalar(
-                out=nsc[:], in0=rsn_v[:, :, 1], scalar1=-1.0 * N, scalar2=0.0, op0=ALU.mult, op1=ALU.add
+                out=nsc[:, :], in0=rsn_v[:, :, 1], scalar1=-1.0 * N, scalar2=0.0, op0=ALU.mult, op1=ALU.add
             )
             st["rho"] = rho
             st["c"] = c
@@ -273,7 +289,7 @@ def tile_layernormgrucell_pa_t_kernel(tc, x, h, W_irz, b_irz, W_hrz, b_hrz, out)
         def s_diag(t):
             dg = dgp.tile([P, P], F32, tag="dg", name="dg")
             nc.gpsimd.tensor_scalar(
-                out=dg[:], in0=ident[:], scalar1=sts[t // 2]["rho"][:, t % 2 : t % 2 + 1], scalar2=0.0, op0=ALU.mult, op1=ALU.add
+                out=dg[:], in0=ident[:], scalar1=sts[gstart[t]]["rho"][:, t - gstart[t] : t - gstart[t] + 1], scalar2=0.0, op0=ALU.mult, op1=ALU.add
             )
             dgs[t] = dg
 
@@ -285,25 +301,17 @@ def tile_layernormgrucell_pa_t_kernel(tc, x, h, W_irz, b_irz, W_hrz, b_hrz, out)
             nc.tensor.matmul(out=ps[:], lhsT=ident[:], rhs=ab[:, 1, cols], start=False, stop=True)
             pss[("j", t, hf)] = ps
 
-        def s_join_g(t):
-            ab = abs_[t]
-            rho = sts[t // 2]["rho"][:, t % 2 : t % 2 + 1]
-            for c0 in range(0, N, GW):
-                cols = slice(c0, c0 + GW)
-                nc.gpsimd.tensor_scalar(out=ab[:, 0, cols], in0=ab[:, 0, cols], scalar1=rho, scalar2=0.0, op0=ALU.mult, op1=ALU.add)
-                nc.gpsimd.tensor_tensor(out=ab[:, 1, cols], in0=ab[:, 0, cols], in1=ab[:, 1, cols], op=ALU.add)
-
         def s_join_v(t):
             ab = abs_[t]
-            rho = sts[t // 2]["rho"][:, t % 2 : t % 2 + 1]
+            rho = sts[gstart[t]]["rho"][:, t - gstart[t] : t - gstart[t] + 1]
             nc.vector.scalar_tensor_tensor(
                 out=ab[:, 1, :], in0=ab[:, 0, :], scalar=rho, in1=ab[:, 1, :], op0=ALU.mult, op1=ALU.add
             )
 
         def s_sig(t):
             ot = op.tile([P, N], F32, tag="ot", name="ot")
-            c_ = sts[t // 2]["c"][:, t % 2 : t % 2 + 1]
-            nsc_ = sts[t // 2]["nsc"][:, t % 2 : t % 2 + 1]
+            c_ = sts[gstart[t]]["c"][:, t - gstart[t] : t - gstart[t] + 1]
+            nsc_ = sts[gstart[t]]["nsc"][:, t - gstart[t] : t - gstart[t] + 1]
             if kind(t) == "P":
                 for hf in range(2):
                     nc.scalar.activation(
@@ -357,18 +365,16 @@ def tile_layernormgrucell_pa_t_kernel(tc, x, h, W_irz, b_irz, W_hrz, b_hrz, out)
                         s_mx(it + 1, o, hf)
             if ok(it + 5):
                 s_tr(it + 5)
-            if it % 2 == 0 and ok(it - 2):
-                s_ch((it - 2) // 2)
-                for t in (it - 2, it - 1):
-                    if kind(t) == "P":
-                        s_diag(t)
-            t = it - LAG + 1
+            for t0 in gsize:
+                if it == t0 + gsize[t0] - 1 + CHD:
+                    s_ch(t0)
+                    for t in range(t0, t0 + gsize[t0]):
+                        if kind(t) == "P":
+                            s_diag(t)
+            t = it - LAG + PJ
             if ok(t) and kind(t) == "P":
                 for hf in range(2):
                     s_join_pe(t, hf)
-            t = it - LAG + 2
-            if ok(t) and kind(t) == "G":
-                s_join_g(t)
             t = it - LAG
             if ok(t) and kind(t) == "V":
                 s_join_v(t)

@@ -7,6 +7,7 @@ F32 = mybir.dt.float32
 BF16 = mybir.dt.bfloat16
 U32 = mybir.dt.uint32
 U8 = mybir.dt.uint8
+I32 = mybir.dt.int32
 FP8X4 = mybir.dt.float8_e4m3fn_x4
 ALU = mybir.AluOpType
 ACT = mybir.ActivationFunctionType
@@ -18,19 +19,28 @@ N = 1024
 NT = B // P
 EPS = 1e-5
 FLOPS = 2 * 2 * B * K * N
-CHUNKS = [(0, 2), (2, 2), (4, 4), (8, 8), (16, 8), (24, 8)]
+CHUNKS = [(0, 4), (4, 4), (8, 8), (16, 8), (24, 8)]
 
-LAG = 7
-HEAD = 2
+LAG = 8
+HEAD = 4
 JOIN = "VVP"
 GROUPS = [4] * 7 + [2, 2]
-PJ = 1
+PJS = ((0, LAG - 1, 1), (1, LAG - 1, 1))
+JVL = LAG
+JPOS = 1
+EVMIN = 6
+BV = "--"
+WV = "----"
+VD = 4
+EVL = 4
 POWW = 8
+VCH = 30
+RSQRT_BITS = 1597463007.0
 CHD = 1
-EVV = "-"
+EVV = "V--"
 EVT = 32
 QB = 1
-AB_BUFS = 10
+AB_BUFS = 11
 
 
 def tile_layernormgrucell_pa_t_kernel(tc, x, h, W_irz, b_irz, W_hrz, b_hrz, out):
@@ -38,12 +48,12 @@ def tile_layernormgrucell_pa_t_kernel(tc, x, h, W_irz, b_irz, W_hrz, b_hrz, out)
     with ExitStack() as ctx:
         const = ctx.enter_context(tc.tile_pool(name="const", bufs=1))
         wgp = ctx.enter_context(tc.tile_pool(name="wgp", bufs=2))
-        xgp = ctx.enter_context(tc.tile_pool(name="xgp", bufs=3))
+        xgp = ctx.enter_context(tc.tile_pool(name="xgp", bufs=EVL))
         xcp = ctx.enter_context(tc.tile_pool(name="xcp", bufs=3))
         abp = ctx.enter_context(tc.tile_pool(name="abp", bufs=AB_BUFS))
-        op = ctx.enter_context(tc.tile_pool(name="op", bufs=4))
+        op = ctx.enter_context(tc.tile_pool(name="op", bufs=3))
         jp = ctx.enter_context(tc.tile_pool(name="jp", bufs=2))
-        stp = ctx.enter_context(tc.tile_pool(name="stp", bufs=AB_BUFS + 2))
+        stp = ctx.enter_context(tc.tile_pool(name="stp", bufs=6))
         dgp = ctx.enter_context(tc.tile_pool(name="dgp", bufs=3))
         psp = ctx.enter_context(tc.psum_pool(name="psp", bufs=8))
         ctx.enter_context(tc.manual_schedule())
@@ -86,10 +96,10 @@ def tile_layernormgrucell_pa_t_kernel(tc, x, h, W_irz, b_irz, W_hrz, b_hrz, out)
 
         load_w(0, 0)
         load_act(0, 0)
-        load_act(1, 0)
+        load_w(0, 1)
         nc.sync.dma_start(out=brow[0:1, 0:N], in_=b_irz.rearrange("(o n) -> o n", o=1))
         nc.sync.dma_start(out=brow[0:1, N : 2 * N], in_=b_hrz.rearrange("(o n) -> o n", o=1))
-        load_w(0, 1)
+        load_act(1, 0)
         load_w(1, 0)
         load_w(1, 1)
         for ci in range(1, len(CHUNKS)):
@@ -98,18 +108,16 @@ def tile_layernormgrucell_pa_t_kernel(tc, x, h, W_irz, b_irz, W_hrz, b_hrz, out)
 
         bias = const.tile([P, 2 * N], BF16, name="bias")
 
-        def spread_bias():
-            for o in range(2):
-                ps = bank(BF16, N)
-                for hf in range(2):
-                    c0 = hf * 512
-                    nc.tensor.matmul(
-                        out=ps[:, c0 : c0 + 512], lhsT=ones[:], rhs=brow[:, o * N + c0 : o * N + c0 + 512], start=True, stop=True
-                    )
-                if o == 0:
-                    nc.vector.tensor_copy(out=bias[:, 0:N], in_=ps[:])
-                else:
-                    nc.scalar.copy(out=bias[:, N : 2 * N], in_=ps[:])
+        def spread_bias(o):
+            ps = bank(BF16, N)
+            for c0 in (0, 512):
+                nc.tensor.matmul(
+                    out=ps[:, c0 : c0 + 512], lhsT=ones[:], rhs=brow[:, o * N + c0 : o * N + c0 + 512], start=True, stop=True
+                )
+            if BV[o] == "V":
+                nc.vector.tensor_copy(out=bias[:, o * N : (o + 1) * N], in_=ps[:])
+            else:
+                nc.scalar.copy(out=bias[:, o * N : (o + 1) * N], in_=ps[:])
 
         wc = [const.tile([P, N], U32, name="wc%d" % o, align_bytes=64) for o in range(2)]
         wsc = [const.tile([P, N], U8, name="wsc%d" % o, align_bytes=64) for o in range(2)]
@@ -182,7 +190,7 @@ def tile_layernormgrucell_pa_t_kernel(tc, x, h, W_irz, b_irz, W_hrz, b_hrz, out)
             s = (t % QB) * 512
             dst = xgs[t // QB][:].bitcast(F32)[:, s : s + 512].rearrange("p (a r u) -> p a r u", a=2, u=2)
             src = tps[t][:].rearrange("p (a u r) -> p a r u", a=2, u=2)
-            if (EVV[t % len(EVV)] == "V" or t >= EVT) and t >= 4:
+            if (EVV[t % len(EVV)] == "V" or t >= EVT) and t >= EVMIN:
                 nc.vector.tensor_copy(out=dst, in_=src)
             else:
                 nc.scalar.copy(out=dst, in_=src)
@@ -195,9 +203,13 @@ def tile_layernormgrucell_pa_t_kernel(tc, x, h, W_irz, b_irz, W_hrz, b_hrz, out)
                 xcs[t // QB] = (xc, xs)
 
         def s_mx(t, o, hf):
-            xc, xs = xcs[t // QB]
             cols = slice(hf * 512, (hf + 1) * 512)
-            c0 = (t % QB) * 256 + o * P
+            if t < HEAD:
+                xc, xs = xcs[("head", o, t // 2)]
+                c0 = (t % 2) * P
+            else:
+                xc, xs = xcs[t // QB]
+                c0 = (t % QB) * 256 + o * P
             ps = bank()
             nc.tensor.matmul_mx(
                 out=ps[:],
@@ -286,6 +298,56 @@ def tile_layernormgrucell_pa_t_kernel(tc, x, h, W_irz, b_irz, W_hrz, b_hrz, out)
             st["c"] = c
             st["nsc"] = nsc
 
+        def s_chv(t0):
+            g = gsize[t0]
+            w = 2 * g
+            st = sts[t0]
+            s0 = st["sv"][:, 0, 0:w]
+            s1 = st["sv"][:, 1, 0:w]
+            tt = nc.vector.tensor_tensor
+            stt = nc.vector.scalar_tensor_tensor
+            dd = small("dd", w)
+            tt(out=dd[:, :], in0=s1, in1=s0, op=ALU.subtract)
+            sm = small("sm", w)
+            tt(out=sm[:, :], in0=s0, in1=s1, op=ALU.add)
+            d2 = small("d2", w)
+            tt(out=d2[:, :], in0=dd[:, :], in1=dd[:, :], op=ALU.mult)
+            qq = small("qq", w)
+            nc.vector.tensor_scalar(
+                out=qq[:, :], in0=st["ss"][:, 0:w], scalar1=1.0 / 256.0, scalar2=EPS * N * N, op0=ALU.mult, op1=ALU.add
+            )
+            vn = small("vn", w)
+            tt(out=vn[:, :], in0=qq[:, :], in1=d2[:, :], op=ALU.subtract)
+            y0 = stp.tile([P, 8], I32, tag="y0", name="y0")
+            nc.vector.tensor_scalar(
+                out=y0[:, 0:w], in0=vn.bitcast(I32), scalar1=-0.5, scalar2=RSQRT_BITS, op0=ALU.mult, op1=ALU.add
+            )
+            y = y0[:, 0:w].bitcast(F32)
+            for k in range(3):
+                ny2 = small("ny2", w)
+                stt(out=ny2[:, :], in0=y, scalar=-0.5, in1=y, op0=ALU.mult, op1=ALU.mult)
+                vy = small("vy", w)
+                tt(out=vy[:, :], in0=ny2[:, :], in1=vn[:, :], op=ALU.mult)
+                yn = small("yn%d" % k, w)
+                stt(out=yn[:, :], in0=vy[:, :], scalar=1.5, in1=y, op0=ALU.add, op1=ALU.mult)
+                y = yn[:, :]
+            y_v = y.rearrange("p (t o) -> p t o", o=2)
+            vn_v = vn[:, :].rearrange("p (t o) -> p t o", o=2)
+            sdn = small("sdn", g)
+            tt(out=sdn[:, :], in0=vn_v[:, :, 1], in1=y_v[:, :, 1], op=ALU.mult)
+            rho = small("rho", g)
+            tt(out=rho[:, :], in0=sdn[:, :], in1=y_v[:, :, 0], op=ALU.mult)
+            mm_ = small("mm_", w)
+            tt(out=mm_[:, :], in0=sm[:, :], in1=y, op=ALU.mult)
+            mm_v = mm_[:, :].rearrange("p (t o) -> p t o", o=2)
+            nsc = small("nsc", g)
+            nc.vector.tensor_scalar(out=nsc[:, :], in0=y_v[:, :, 1], scalar1=-1.0 * N, scalar2=0.0, op0=ALU.mult, op1=ALU.add)
+            c = small("c", g)
+            tt(out=c[:, :], in0=mm_v[:, :, 0], in1=mm_v[:, :, 1], op=ALU.add)
+            st["rho"] = rho
+            st["c"] = c
+            st["nsc"] = nsc
+
         def s_diag(t):
             dg = dgp.tile([P, P], F32, tag="dg", name="dg")
             nc.gpsimd.tensor_scalar(
@@ -321,68 +383,137 @@ def tile_layernormgrucell_pa_t_kernel(tc, x, h, W_irz, b_irz, W_hrz, b_hrz, out)
                 nc.scalar.activation(out=ot[:], in_=abs_[t][:, 1, :], func=ACT.Sigmoid, bias=c_, scale=nsc_)
             nc.sync.dma_start(out=out.rearrange("(p t) j -> p t j", t=NT)[:, t, :], in_=ot[:])
 
-        w_transpose(0, 0, True)
-        w_quantise(0, 0)
-        for t in range(HEAD):
-            s_tr(t)
-            s_ev(t)
-            s_q(t)
-        if QB == 2:
-            s_q(0)
-        spread_bias()
-        w_transpose(0, 1, False)
-        for (o, hf) in ((0, 0), (0, 1), (1, 0), (1, 1)):
-            for t in range(HEAD):
-                s_mx(t, o, hf)
-            for t in range(HEAD):
-                s_p1(t, o, hf)
-            if (o, hf) == (0, 0):
-                w_quantise(0, 1)
-                w_transpose(1, 0, False)
-            if (o, hf) == (0, 1):
-                w_quantise(1, 0)
-                w_transpose(1, 1, False)
-            if (o, hf) == (1, 0):
-                w_quantise(1, 1)
-                for t in range(HEAD):
-                    s_sq(t, 0)
-                for t in (2, 3):
-                    s_tr(t)
-                    s_ev(t)
-        s_q(2)
-        s_tr(4)
+        heads = {}
 
-        for it in range(NT + LAG):
-            if ok(it + 2) and it + 2 > HEAD:
-                s_q(it + 2)
-            if ok(it) and it >= HEAD:
-                for o in range(2):
-                    for hf in range(2):
-                        s_p1(it, o, hf)
-            if ok(it + 1) and it + 1 >= HEAD:
-                for o in range(2):
-                    for hf in range(2):
-                        s_mx(it + 1, o, hf)
-            if ok(it + 5):
-                s_tr(it + 5)
+        def h_tr(o, pr):
+            tp = bank()
+            for a in range(2):
+                w_ = act_words(o, 2 * pr + a)
+                for u in range(2):
+                    q = 2 * a + u
+                    nc.tensor.transpose(tp[:, q * P : (q + 1) * P], w_[:, u:256:2], ident[:])
+            heads[(o, pr)] = tp
+
+        def h_ev(o, pr):
+            xg = xgp.tile([P, 1024], BF16, tag="xg", name="xg", align_bytes=64)
+            dst = xg[:].bitcast(F32).rearrange("p (a r u) -> p a r u", a=2, u=2)
+            nc.scalar.copy(out=dst, in_=heads[(o, pr)][:].rearrange("p (a u r) -> p a r u", a=2, u=2))
+            heads[(o, pr)] = xg
+
+        def h_q(o, pr):
+            xc = const.tile([P, 256], U32, name="hxc%d%d" % (o, pr), align_bytes=64)
+            xs = const.tile([P, 256], U8, name="hxs%d%d" % (o, pr), align_bytes=64)
+            nc.vector.quantize_mx(out=xc[:].bitcast(FP8X4), scales=xs[:], in_=heads[(o, pr)][:])
+            xcs[("head", o, pr)] = (xc, xs)
+
+        def act_ready(ts):
+            for t in ts:
+                s_tr(t)
+            for t in ts:
+                s_ev(t)
+
+        def mxs(ts, o, hf):
+            for t in ts:
+                s_mx(t, o, hf)
+
+        def p1s(ts, o, hf):
+            for t in ts:
+                s_p1(t, o, hf)
+
+        def sqs(ts, o):
+            for t in ts:
+                s_sq(t, o)
+
+        first, second, four = (0, 1), (2, 3), (0, 1, 2, 3)
+        w_transpose(0, 0, WV[0] == "V")
+        w_quantise(0, 0)
+        h_tr(0, 0)
+        h_ev(0, 0)
+        h_q(0, 0)
+        h_tr(0, 1)
+        spread_bias(0)
+        h_ev(0, 1)
+        mxs(first, 0, 0)
+        p1s(first, 0, 0)
+        h_q(0, 1)
+        w_transpose(0, 1, WV[1] == "V")
+        mxs(second, 0, 0)
+        p1s(second, 0, 0)
+        w_quantise(0, 1)
+        h_tr(1, 0)
+        h_ev(1, 0)
+        h_tr(1, 1)
+        h_ev(1, 1)
+        spread_bias(1)
+        w_transpose(1, 0, WV[2] == "V")
+        mxs(four, 0, 1)
+        p1s(first, 0, 1)
+        h_q(1, 0)
+        w_quantise(1, 0)
+        p1s(second, 0, 1)
+        h_q(1, 1)
+        sqs(first, 0)
+        w_transpose(1, 1, WV[3] == "V")
+        mxs(four, 1, 0)
+        p1s(first, 1, 0)
+        w_quantise(1, 1)
+        p1s(second, 1, 0)
+        sqs(second, 0)
+        act_ready((4, 5))
+        mxs(four, 1, 1)
+        s_q(4)
+        p1s(first, 1, 1)
+        s_q(5)
+        p1s(second, 1, 1)
+        sqs(first, 1)
+        act_ready((6,))
+        sqs(second, 1)
+        for t in range(7, EVL + 4):
+            act_ready((t,))
+        s_tr(EVL + 4)
+        for o in range(2):
+            for hf in range(2):
+                s_mx(4, o, hf)
+
+        def chain_at(it):
             for t0 in gsize:
-                if it == t0 + gsize[t0] - 1 + CHD:
-                    s_ch(t0)
+                if it == t0 + gsize[t0] - 1 + CHD + (VD if t0 >= VCH else 0):
+                    if t0 >= VCH:
+                        s_chv(t0)
+                    else:
+                        s_ch(t0)
                     for t in range(t0, t0 + gsize[t0]):
                         if kind(t) == "P":
                             s_diag(t)
-            t = it - LAG + PJ
-            if ok(t) and kind(t) == "P":
-                for hf in range(2):
-                    s_join_pe(t, hf)
-            t = it - LAG
-            if ok(t) and kind(t) == "V":
-                s_join_v(t)
+
+        for it in range(HEAD):
+            chain_at(it)
+
+        for it in range(HEAD, NT + LAG):
+            chain_at(it)
+            if ok(it + 2):
+                s_q(it + 2)
+            for o in range(2):
+                if ok(it):
+                    for hf in range(2):
+                        s_p1(it, o, hf)
+                t = it - JVL
+                if o == JPOS and ok(t) and kind(t) == "V":
+                    s_join_v(t)
+            for o in range(2):
+                if ok(it + 1):
+                    for hf in range(2):
+                        s_mx(it + 1, o, hf)
+                for (hf, lag, pos) in PJS:
+                    t = it - lag
+                    if ok(t) and kind(t) == "P" and pos == o:
+                        s_join_pe(t, hf)
+            if ok(it + EVL + 1):
+                s_tr(it + EVL + 1)
             if ok(it):
-                if it >= HEAD:
-                    s_sq(it, 0)
+                s_sq(it, 0)
                 s_sq(it, 1)
             if ok(it - LAG):
                 s_sig(it - LAG)
-            if ok(it + 4):
-                s_ev(it + 4)
+            if ok(it + EVL):
+                s_ev(it + EVL)

@@ -19,25 +19,28 @@ N = 1024
 NT = B // P
 EPS = 1e-5
 FLOPS = 2 * 2 * B * K * N
-CHUNKS = [(0, 4), (4, 4), (8, 8), (16, 8), (24, 8)]
+CHUNKS = [(0, 2), (2, 2)] + [(t0, 4) for t0 in range(4, 32, 4)]
+ACT_BUFS = 6
+OT = 5
 
 LAG = 8
 HEAD = 4
 JOIN = "VVP"
-GROUPS = [4] * 7 + [2, 2]
-PJS = ((0, LAG - 1, 1), (1, LAG - 1, 1))
-JVL = LAG
+GROUPS = [4] * 6 + [2, 2, 2, 2]
+PJS = ((0, 2, 2), (1, 1, 2))
 JPOS = 1
 EVMIN = 6
 BV = "--"
 WV = "----"
-VD = 4
+WS = 2
+LW = 512
+VD = 2
 EVL = 4
 POWW = 8
 VCH = 30
 RSQRT_BITS = 1597463007.0
 CHD = 1
-EVV = "V--"
+EVV = "V-"
 EVT = 32
 QB = 1
 AB_BUFS = 11
@@ -47,11 +50,12 @@ def tile_layernormgrucell_pa_t_kernel(tc, x, h, W_irz, b_irz, W_hrz, b_hrz, out)
     nc = tc.nc
     with ExitStack() as ctx:
         const = ctx.enter_context(tc.tile_pool(name="const", bufs=1))
+        actp = ctx.enter_context(tc.tile_pool(name="actp", bufs=ACT_BUFS))
         wgp = ctx.enter_context(tc.tile_pool(name="wgp", bufs=2))
         xgp = ctx.enter_context(tc.tile_pool(name="xgp", bufs=EVL))
         xcp = ctx.enter_context(tc.tile_pool(name="xcp", bufs=3))
         abp = ctx.enter_context(tc.tile_pool(name="abp", bufs=AB_BUFS))
-        op = ctx.enter_context(tc.tile_pool(name="op", bufs=3))
+        op = ctx.enter_context(tc.tile_pool(name="op", bufs=OT))
         jp = ctx.enter_context(tc.tile_pool(name="jp", bufs=2))
         stp = ctx.enter_context(tc.tile_pool(name="stp", bufs=6))
         dgp = ctx.enter_context(tc.tile_pool(name="dgp", bufs=3))
@@ -79,7 +83,7 @@ def tile_layernormgrucell_pa_t_kernel(tc, x, h, W_irz, b_irz, W_hrz, b_hrz, out)
 
         def load_act(o, ci):
             t0, nt = CHUNKS[ci]
-            t_ = const.tile([P, nt * K], BF16, name="act%d_%d" % (o, ci))
+            t_ = actp.tile([P, nt * K], BF16, tag="act%d" % o, name="act%d" % o)
             nc.sync.dma_start(
                 out=t_[:].rearrange("p (t k) -> p t k", k=K),
                 in_=acts[o].rearrange("(p t) k -> p t k", t=NT)[:, t0 : t0 + nt, :],
@@ -88,21 +92,26 @@ def tile_layernormgrucell_pa_t_kernel(tc, x, h, W_irz, b_irz, W_hrz, b_hrz, out)
 
         def load_w(o, hf):
             t_ = const.tile([P, 4 * K], BF16, name="wraw%d_%d" % (o, hf))
-            nc.sync.dma_start(
-                out=t_[:].rearrange("p (j k) -> p j k", k=K),
-                in_=wts[o][hf * 512 : (hf + 1) * 512, :].rearrange("(j p) k -> p j k", p=P),
-            )
+            step = 4 if (o, hf) != (0, 0) else WS
+            for j in range(0, 4, step):
+                r0 = hf * 512 + j * P
+                nc.sync.dma_start(
+                    out=t_[:, j * K : (j + step) * K].rearrange("p (j k) -> p j k", k=K),
+                    in_=wts[o][r0 : r0 + step * P, :].rearrange("(j p) k -> p j k", p=P),
+                )
             wraw[o][hf] = t_
 
         load_w(0, 0)
-        load_act(0, 0)
-        load_w(0, 1)
         nc.sync.dma_start(out=brow[0:1, 0:N], in_=b_irz.rearrange("(o n) -> o n", o=1))
+        load_act(0, 0)
+        load_act(0, 1)
+        load_w(0, 1)
         nc.sync.dma_start(out=brow[0:1, N : 2 * N], in_=b_hrz.rearrange("(o n) -> o n", o=1))
         load_act(1, 0)
+        load_act(1, 1)
         load_w(1, 0)
         load_w(1, 1)
-        for ci in range(1, len(CHUNKS)):
+        for ci in range(2, len(CHUNKS)):
             load_act(0, ci)
             load_act(1, ci)
 
@@ -335,13 +344,13 @@ def tile_layernormgrucell_pa_t_kernel(tc, x, h, W_irz, b_irz, W_hrz, b_hrz, out)
             vn_v = vn[:, :].rearrange("p (t o) -> p t o", o=2)
             sdn = small("sdn", g)
             tt(out=sdn[:, :], in0=vn_v[:, :, 1], in1=y_v[:, :, 1], op=ALU.mult)
-            rho = small("rho", g)
-            tt(out=rho[:, :], in0=sdn[:, :], in1=y_v[:, :, 0], op=ALU.mult)
             mm_ = small("mm_", w)
             tt(out=mm_[:, :], in0=sm[:, :], in1=y, op=ALU.mult)
             mm_v = mm_[:, :].rearrange("p (t o) -> p t o", o=2)
             nsc = small("nsc", g)
             nc.vector.tensor_scalar(out=nsc[:, :], in0=y_v[:, :, 1], scalar1=-1.0 * N, scalar2=0.0, op0=ALU.mult, op1=ALU.add)
+            rho = small("rho", g)
+            tt(out=rho[:, :], in0=sdn[:, :], in1=y_v[:, :, 0], op=ALU.mult)
             c = small("c", g)
             tt(out=c[:, :], in0=mm_v[:, :, 0], in1=mm_v[:, :, 1], op=ALU.add)
             st["rho"] = rho
@@ -372,6 +381,7 @@ def tile_layernormgrucell_pa_t_kernel(tc, x, h, W_irz, b_irz, W_hrz, b_hrz, out)
 
         def s_sig(t):
             ot = op.tile([P, N], F32, tag="ot", name="ot")
+            w = LW if t == NT - 1 else N
             c_ = sts[gstart[t]]["c"][:, t - gstart[t] : t - gstart[t] + 1]
             nsc_ = sts[gstart[t]]["nsc"][:, t - gstart[t] : t - gstart[t] + 1]
             if kind(t) == "P":
@@ -380,8 +390,12 @@ def tile_layernormgrucell_pa_t_kernel(tc, x, h, W_irz, b_irz, W_hrz, b_hrz, out)
                         out=ot[:, hf * 512 : (hf + 1) * 512], in_=pss[("j", t, hf)][:], func=ACT.Sigmoid, bias=c_, scale=nsc_
                     )
             else:
-                nc.scalar.activation(out=ot[:], in_=abs_[t][:, 1, :], func=ACT.Sigmoid, bias=c_, scale=nsc_)
-            nc.sync.dma_start(out=out.rearrange("(p t) j -> p t j", t=NT)[:, t, :], in_=ot[:])
+                for c0 in range(0, N, w):
+                    nc.scalar.activation(
+                        out=ot[:, c0 : c0 + w], in_=abs_[t][:, 1, c0 : c0 + w], func=ACT.Sigmoid, bias=c_, scale=nsc_
+                    )
+            for c0 in range(0, N, w):
+                nc.sync.dma_start(out=out.rearrange("(p t) j -> p t j", t=NT)[:, t, c0 : c0 + w], in_=ot[:, c0 : c0 + w])
 
         heads = {}
 
@@ -475,6 +489,12 @@ def tile_layernormgrucell_pa_t_kernel(tc, x, h, W_irz, b_irz, W_hrz, b_hrz, out)
             for hf in range(2):
                 s_mx(4, o, hf)
 
+        def lag(t):
+            return LAG
+
+        def due(it, early=0):
+            return [t for t in range(NT) if t + lag(t) - early == it]
+
         def chain_at(it):
             for t0 in gsize:
                 if it == t0 + gsize[t0] - 1 + CHD + (VD if t0 >= VCH else 0):
@@ -489,6 +509,13 @@ def tile_layernormgrucell_pa_t_kernel(tc, x, h, W_irz, b_irz, W_hrz, b_hrz, out)
         for it in range(HEAD):
             chain_at(it)
 
+        def joins(it, pos):
+            for (hf, early, pos_) in PJS:
+                if pos == pos_:
+                    for t in due(it, early):
+                        if kind(t) == "P":
+                            s_join_pe(t, hf)
+
         for it in range(HEAD, NT + LAG):
             chain_at(it)
             if ok(it + 2):
@@ -497,23 +524,22 @@ def tile_layernormgrucell_pa_t_kernel(tc, x, h, W_irz, b_irz, W_hrz, b_hrz, out)
                 if ok(it):
                     for hf in range(2):
                         s_p1(it, o, hf)
-                t = it - JVL
-                if o == JPOS and ok(t) and kind(t) == "V":
-                    s_join_v(t)
+                if o == JPOS:
+                    for t in due(it):
+                        if kind(t) == "V":
+                            s_join_v(t)
             for o in range(2):
                 if ok(it + 1):
                     for hf in range(2):
                         s_mx(it + 1, o, hf)
-                for (hf, lag, pos) in PJS:
-                    t = it - lag
-                    if ok(t) and kind(t) == "P" and pos == o:
-                        s_join_pe(t, hf)
+                joins(it, o)
             if ok(it + EVL + 1):
                 s_tr(it + EVL + 1)
+            joins(it, 2)
             if ok(it):
                 s_sq(it, 0)
                 s_sq(it, 1)
-            if ok(it - LAG):
-                s_sig(it - LAG)
+            for t in due(it):
+                s_sig(t)
             if ok(it + EVL):
                 s_ev(it + EVL)

@@ -35,12 +35,12 @@ WV = "----"
 WS = 2
 LW = 512
 VD = 2
-EVL = 4
+EVL = 5
 POWW = 8
 VCH = 30
 RSQRT_BITS = 1597463007.0
 CHD = 1
-EVV = "V-"
+EVV = "V--"
 EVT = 32
 QB = 1
 AB_BUFS = 11
@@ -193,7 +193,7 @@ def tile_layernormgrucell_pa_t_kernel(tc, x, h, W_irz, b_irz, W_hrz, b_hrz, out)
             tps[t] = tp
 
         def s_ev(t):
-            if t % QB == 0:
+            if t % QB == 0 or t // QB not in xgs:
                 xg = xgp.tile([P, QB * 1024], BF16, tag="xg", name="xg", align_bytes=64)
                 xgs[t // QB] = xg
             s = (t % QB) * 512
@@ -439,7 +439,7 @@ def tile_layernormgrucell_pa_t_kernel(tc, x, h, W_irz, b_irz, W_hrz, b_hrz, out)
                 s_sq(t, o)
 
         first, second, four = (0, 1), (2, 3), (0, 1, 2, 3)
-        w_transpose(0, 0, WV[0] == "V")
+        w_transpose(0, 0, False)
         w_quantise(0, 0)
         h_tr(0, 0)
         h_ev(0, 0)
@@ -448,18 +448,18 @@ def tile_layernormgrucell_pa_t_kernel(tc, x, h, W_irz, b_irz, W_hrz, b_hrz, out)
         spread_bias(0)
         h_ev(0, 1)
         mxs(first, 0, 0)
-        p1s(first, 0, 0)
         h_q(0, 1)
-        w_transpose(0, 1, WV[1] == "V")
+        p1s(first, 0, 0)
+        w_transpose(0, 1, False)
+        h_tr(1, 0)
         mxs(second, 0, 0)
         p1s(second, 0, 0)
         w_quantise(0, 1)
-        h_tr(1, 0)
         h_ev(1, 0)
         h_tr(1, 1)
         h_ev(1, 1)
+        w_transpose(1, 0, False)
         spread_bias(1)
-        w_transpose(1, 0, WV[2] == "V")
         mxs(four, 0, 1)
         p1s(first, 0, 1)
         h_q(1, 0)
@@ -467,7 +467,7 @@ def tile_layernormgrucell_pa_t_kernel(tc, x, h, W_irz, b_irz, W_hrz, b_hrz, out)
         p1s(second, 0, 1)
         h_q(1, 1)
         sqs(first, 0)
-        w_transpose(1, 1, WV[3] == "V")
+        w_transpose(1, 1, False)
         mxs(four, 1, 0)
         p1s(first, 1, 0)
         w_quantise(1, 1)
@@ -477,7 +477,8 @@ def tile_layernormgrucell_pa_t_kernel(tc, x, h, W_irz, b_irz, W_hrz, b_hrz, out)
         mxs(four, 1, 1)
         s_q(4)
         p1s(first, 1, 1)
-        s_q(5)
+        if QB == 1:
+            s_q(5)
         p1s(second, 1, 1)
         sqs(first, 1)
         act_ready((6,))

@@ -26,7 +26,7 @@ OT = 5
 LAG = 8
 HEAD = 4
 JOIN = "VVP"
-GROUPS = [4] * 6 + [2, 2, 2, 2]
+GROUPS = [3] * 10 + [2]
 PJS = ((0, 2, 2), (1, 1, 2))
 JPOS = 1
 EVMIN = 6

@@ -22,6 +22,7 @@ FLOPS = 2 * 2 * B * K * N
 CHUNKS = [(0, 2), (2, 2)] + [(t0, 4) for t0 in range(4, 32, 4)]
 ACT_BUFS = 6
 OT = 5
+WARM = (3, 0)
 
 LAG = 8
 HEAD = 4
@@ -30,18 +31,22 @@ GROUPS = [3] * 10 + [2]
 PJS = ((0, 2, 2), (1, 1, 2))
 JPOS = 1
 EVMIN = 6
-BV = "--"
+BV = "V-"
 WV = "----"
 WS = 2
 LW = 512
-VD = 2
+VD = 5
 EVL = 5
 POWW = 8
 VCH = 30
 RSQRT_BITS = 1597463007.0
 CHD = 1
 EVV = "V--"
-EVT = 32
+VORD = "abqje"
+PORD = "abt01"
+SORD = "01se"
+PJE = (2, 1)
+QL = 2
 QB = 1
 AB_BUFS = 11
 
@@ -67,12 +72,14 @@ def tile_layernormgrucell_pa_t_kernel(tc, x, h, W_irz, b_irz, W_hrz, b_hrz, out)
 
         ident = const.tile([P, P], F32, name="ident")
         make_identity(nc, ident[:])
-        brow = const.tile([P, 2 * N], BF16, name="brow")
-        nc.vector.memset(brow[:].bitcast(mybir.dt.int32), 0)
         ones = const.tile([P, P], BF16, name="ones")
         nc.vector.memset(ones[:], 1.0)
+        idle = const.tile([P, 512], BF16, name="idle")
+        nc.vector.memset(idle[:].bitcast(I32), 0)
         mhalf = const.tile([P, 8], F32, name="mhalf")
         nc.vector.memset(mhalf[:], -0.5)
+        brow = const.tile([P, 2 * N], BF16, name="brow")
+        nc.vector.memset(brow[:].bitcast(I32), 0)
         warm = const.tile([P, 1], F32, name="warm")
         nc.scalar.activation(out=warm[:], in_=mhalf[:, 0:1], func=ACT.Sigmoid)
 
@@ -102,8 +109,8 @@ def tile_layernormgrucell_pa_t_kernel(tc, x, h, W_irz, b_irz, W_hrz, b_hrz, out)
             wraw[o][hf] = t_
 
         load_w(0, 0)
-        nc.sync.dma_start(out=brow[0:1, 0:N], in_=b_irz.rearrange("(o n) -> o n", o=1))
         load_act(0, 0)
+        nc.sync.dma_start(out=brow[0:1, 0:N], in_=b_irz.rearrange("(o n) -> o n", o=1))
         load_act(0, 1)
         load_w(0, 1)
         nc.sync.dma_start(out=brow[0:1, N : 2 * N], in_=b_hrz.rearrange("(o n) -> o n", o=1))
@@ -199,7 +206,7 @@ def tile_layernormgrucell_pa_t_kernel(tc, x, h, W_irz, b_irz, W_hrz, b_hrz, out)
             s = (t % QB) * 512
             dst = xgs[t // QB][:].bitcast(F32)[:, s : s + 512].rearrange("p (a r u) -> p a r u", a=2, u=2)
             src = tps[t][:].rearrange("p (a u r) -> p a r u", a=2, u=2)
-            if (EVV[t % len(EVV)] == "V" or t >= EVT) and t >= EVMIN:
+            if EVV[t % len(EVV)] == "V" and t >= EVMIN:
                 nc.vector.tensor_copy(out=dst, in_=src)
             else:
                 nc.scalar.copy(out=dst, in_=src)
@@ -438,8 +445,17 @@ def tile_layernormgrucell_pa_t_kernel(tc, x, h, W_irz, b_irz, W_hrz, b_hrz, out)
             for t in ts:
                 s_sq(t, o)
 
+        def keep_warm(n):
+            ps = bank()
+            for k in range(n):
+                nc.tensor.matmul(out=ps[:], lhsT=ones[:], rhs=idle[:], start=True, stop=True)
+
         first, second, four = (0, 1), (2, 3), (0, 1, 2, 3)
+        if WARM[0]:
+            keep_warm(WARM[0])
         w_transpose(0, 0, False)
+        if WARM[1]:
+            keep_warm(WARM[1])
         w_quantise(0, 0)
         h_tr(0, 0)
         h_ev(0, 0)
@@ -517,30 +533,38 @@ def tile_layernormgrucell_pa_t_kernel(tc, x, h, W_irz, b_irz, W_hrz, b_hrz, out)
                         if kind(t) == "P":
                             s_join_pe(t, hf)
 
+        def ev_on_vector(t):
+            return t >= EVMIN and EVV[t % len(EVV)] == "V"
+
         for it in range(HEAD, NT + LAG):
             chain_at(it)
-            if ok(it + 2):
-                s_q(it + 2)
-            for o in range(2):
-                if ok(it):
+            for k_ in VORD:
+                if k_ == "q" and ok(it + QL):
+                    s_q(it + QL)
+                if k_ in "ab" and ok(it):
                     for hf in range(2):
-                        s_p1(it, o, hf)
-                if o == JPOS:
+                        s_p1(it, "ab".index(k_), hf)
+                if k_ == "j":
                     for t in due(it):
                         if kind(t) == "V":
                             s_join_v(t)
-            for o in range(2):
-                if ok(it + 1):
+                if k_ == "e" and ok(it + EVL) and ev_on_vector(it + EVL):
+                    s_ev(it + EVL)
+            for k_ in PORD:
+                if k_ in "ab" and ok(it + 1):
                     for hf in range(2):
-                        s_mx(it + 1, o, hf)
-                joins(it, o)
-            if ok(it + EVL + 1):
-                s_tr(it + EVL + 1)
-            joins(it, 2)
-            if ok(it):
-                s_sq(it, 0)
-                s_sq(it, 1)
-            for t in due(it):
-                s_sig(t)
-            if ok(it + EVL):
-                s_ev(it + EVL)
+                        s_mx(it + 1, "ab".index(k_), hf)
+                if k_ == "t" and ok(it + EVL + 1):
+                    s_tr(it + EVL + 1)
+                if k_ in "01":
+                    for t in due(it, PJE[int(k_)]):
+                        if kind(t) == "P":
+                            s_join_pe(t, int(k_))
+            for k_ in SORD:
+                if k_ in "01" and ok(it):
+                    s_sq(it, int(k_))
+                if k_ == "s":
+                    for t in due(it):
+                        s_sig(t)
+                if k_ == "e" and ok(it + EVL) and not ev_on_vector(it + EVL):
+                    s_ev(it + EVL)

from contextlib import ExitStack

import concourse.mybir as mybir
from concourse.masks import make_identity

F32 = mybir.dt.float32
BF16 = mybir.dt.bfloat16
U32 = mybir.dt.uint32
U8 = mybir.dt.uint8
I32 = mybir.dt.int32
FP8X4 = mybir.dt.float8_e4m3fn_x4
ALU = mybir.AluOpType
ACT = mybir.ActivationFunctionType

P = 128
B = 4096
K = 512
N = 1024
NT = B // P
EPS = 1e-5
FLOPS = 2 * 2 * B * K * N
CHUNKS = [(0, 2), (2, 2)] + [(t0, 4) for t0 in range(4, 32, 4)]
ACT_BUFS = 6
OT = 5
WARM = (3, 0)

LAG = 8
HEAD = 4
JOIN = "VVP"
GROUPS = [3] * 10 + [2]
PJS = ((0, 2, 2), (1, 1, 2))
JPOS = 1
EVMIN = 6
BV = "V-"
WV = "----"
WS = 2
LW = 512
VD = 5
EVL = 5
POWW = 8
VCH = 30
RSQRT_BITS = 1597463007.0
CHD = 1
EVV = "V--"
VORD = "abqje"
PORD = "abt01"
SORD = "01se"
PJE = (2, 1)
QL = 2
QB = 1
AB_BUFS = 11


def tile_layernormgrucell_pa_t_kernel(tc, x, h, W_irz, b_irz, W_hrz, b_hrz, out):
    nc = tc.nc
    with ExitStack() as ctx:
        const = ctx.enter_context(tc.tile_pool(name="const", bufs=1))
        actp = ctx.enter_context(tc.tile_pool(name="actp", bufs=ACT_BUFS))
        wgp = ctx.enter_context(tc.tile_pool(name="wgp", bufs=2))
        xgp = ctx.enter_context(tc.tile_pool(name="xgp", bufs=EVL))
        xcp = ctx.enter_context(tc.tile_pool(name="xcp", bufs=3))
        abp = ctx.enter_context(tc.tile_pool(name="abp", bufs=AB_BUFS))
        op = ctx.enter_context(tc.tile_pool(name="op", bufs=OT))
        jp = ctx.enter_context(tc.tile_pool(name="jp", bufs=2))
        stp = ctx.enter_context(tc.tile_pool(name="stp", bufs=6))
        dgp = ctx.enter_context(tc.tile_pool(name="dgp", bufs=3))
        psp = ctx.enter_context(tc.psum_pool(name="psp", bufs=8))
        ctx.enter_context(tc.manual_schedule())

        def bank(dt=F32, width=512):
            return psp.tile([P, width], dt, tag="bank", name="bank")

        ident = const.tile([P, P], F32, name="ident")
        make_identity(nc, ident[:])
        ones = const.tile([P, P], BF16, name="ones")
        nc.vector.memset(ones[:], 1.0)
        idle = const.tile([P, 512], BF16, name="idle")
        nc.vector.memset(idle[:].bitcast(I32), 0)
        mhalf = const.tile([P, 8], F32, name="mhalf")
        nc.vector.memset(mhalf[:], -0.5)
        brow = const.tile([P, 2 * N], BF16, name="brow")
        nc.vector.memset(brow[:].bitcast(I32), 0)
        warm = const.tile([P, 1], F32, name="warm")
        nc.scalar.activation(out=warm[:], in_=mhalf[:, 0:1], func=ACT.Sigmoid)

        acts = (x, h)
        wts = (W_irz, W_hrz)
        xch = [[None] * len(CHUNKS), [None] * len(CHUNKS)]
        wraw = [[None, None], [None, None]]

        def load_act(o, ci):
            t0, nt = CHUNKS[ci]
            t_ = actp.tile([P, nt * K], BF16, tag="act%d" % o, name="act%d" % o)
            nc.sync.dma_start(
                out=t_[:].rearrange("p (t k) -> p t k", k=K),
                in_=acts[o].rearrange("(p t) k -> p t k", t=NT)[:, t0 : t0 + nt, :],
            )
            xch[o][ci] = t_

        def load_w(o, hf):
            t_ = const.tile([P, 4 * K], BF16, name="wraw%d_%d" % (o, hf))
            step = 4 if (o, hf) != (0, 0) else WS
            for j in range(0, 4, step):
                r0 = hf * 512 + j * P
                nc.sync.dma_start(
                    out=t_[:, j * K : (j + step) * K].rearrange("p (j k) -> p j k", k=K),
                    in_=wts[o][r0 : r0 + step * P, :].rearrange("(j p) k -> p j k", p=P),
                )
            wraw[o][hf] = t_

        load_w(0, 0)
        load_act(0, 0)
        nc.sync.dma_start(out=brow[0:1, 0:N], in_=b_irz.rearrange("(o n) -> o n", o=1))
        load_act(0, 1)
        load_w(0, 1)
        nc.sync.dma_start(out=brow[0:1, N : 2 * N], in_=b_hrz.rearrange("(o n) -> o n", o=1))
        load_act(1, 0)
        load_act(1, 1)
        load_w(1, 0)
        load_w(1, 1)
        for ci in range(2, len(CHUNKS)):
            load_act(0, ci)
            load_act(1, ci)

        bias = const.tile([P, 2 * N], BF16, name="bias")

        def spread_bias(o):
            ps = bank(BF16, N)
            for c0 in (0, 512):
                nc.tensor.matmul(
                    out=ps[:, c0 : c0 + 512], lhsT=ones[:], rhs=brow[:, o * N + c0 : o * N + c0 + 512], start=True, stop=True
                )
            if BV[o] == "V":
                nc.vector.tensor_copy(out=bias[:, o * N : (o + 1) * N], in_=ps[:])
            else:
                nc.scalar.copy(out=bias[:, o * N : (o + 1) * N], in_=ps[:])

        wc = [const.tile([P, N], U32, name="wc%d" % o, align_bytes=64) for o in range(2)]
        wsc = [const.tile([P, N], U8, name="wsc%d" % o, align_bytes=64) for o in range(2)]
        wgs = {}

        def w_transpose(o, hf, second_on_vector):
            raw_w = wraw[o][hf][:].bitcast(F32)
            wg = wgp.tile([P, 2048], BF16, tag="wg", name="wg", align_bytes=64)
            wg_w = wg[:].bitcast(F32)
            for pr in range(2):
                tp = bank()
                for q in range(4):
                    c0 = pr * 512 + (q // 2) * 256
                    nc.tensor.transpose(tp[:, q * P : (q + 1) * P], raw_w[:, c0 + q % 2 : c0 + 256 : 2], ident[:])
                dst = wg_w[:, pr * 512 : (pr + 1) * 512].rearrange("p (a r u) -> p a r u", a=2, u=2)
                src = tp[:].rearrange("p (a u r) -> p a r u", a=2, u=2)
                if pr == 1 and second_on_vector:
                    nc.vector.tensor_copy(out=dst, in_=src)
                else:
                    nc.scalar.copy(out=dst, in_=src)
            wgs[(o, hf)] = wg

        def w_quantise(o, hf):
            cols = slice(hf * 512, (hf + 1) * 512)
            nc.vector.quantize_mx(out=wc[o][:, cols].bitcast(FP8X4), scales=wsc[o][:, cols], in_=wgs[(o, hf)][:])

        def act_words(o, t):
            for ci in range(len(CHUNKS)):
                t0, nt = CHUNKS[ci]
                if t0 <= t < t0 + nt:
                    return xch[o][ci][:].bitcast(F32)[:, (t - t0) * 256 : (t - t0 + 1) * 256]
            raise ValueError("no chunk")

        dgs = {}
        tps = {}
        xgs = {}
        xcs = {}
        pss = {}
        abs_ = {}
        sts = {}

        gsize = {}
        gstart = {}
        t0_ = 0
        for g_ in GROUPS:
            gsize[t0_] = g_
            for t in range(t0_, t0_ + g_):
                gstart[t] = t0_
            t0_ += g_

        def ok(t):
            return 0 <= t < NT

        def kind(t):
            return JOIN[t % len(JOIN)]

        def s_tr(t):
            tp = bank()
            for o in range(2):
                w_ = act_words(o, t)
                for u in range(2):
                    q = 2 * o + u
                    nc.tensor.transpose(tp[:, q * P : (q + 1) * P], w_[:, u:256:2], ident[:])
            tps[t] = tp

        def s_ev(t):
            if t % QB == 0 or t // QB not in xgs:
                xg = xgp.tile([P, QB * 1024], BF16, tag="xg", name="xg", align_bytes=64)
                xgs[t // QB] = xg
            s = (t % QB) * 512
            dst = xgs[t // QB][:].bitcast(F32)[:, s : s + 512].rearrange("p (a r u) -> p a r u", a=2, u=2)
            src = tps[t][:].rearrange("p (a u r) -> p a r u", a=2, u=2)
            if EVV[t % len(EVV)] == "V" and t >= EVMIN:
                nc.vector.tensor_copy(out=dst, in_=src)
            else:
                nc.scalar.copy(out=dst, in_=src)

        def s_q(t):
            if t % QB == 0:
                xc = xcp.tile([P, QB * 256], U32, tag="xc", name="xc", align_bytes=64)
                xs = xcp.tile([P, QB * 256], U8, tag="xs", name="xs", align_bytes=64)
                nc.vector.quantize_mx(out=xc[:].bitcast(FP8X4), scales=xs[:], in_=xgs[t // QB][:])
                xcs[t // QB] = (xc, xs)

        def s_mx(t, o, hf):
            cols = slice(hf * 512, (hf + 1) * 512)
            if t < HEAD:
                xc, xs = xcs[("head", o, t // 2)]
                c0 = (t % 2) * P
            else:
                xc, xs = xcs[t // QB]
                c0 = (t % QB) * 256 + o * P
            ps = bank()
            nc.tensor.matmul_mx(
                out=ps[:],
                lhsT=xc[:, c0 : c0 + P].bitcast(FP8X4),
                lhsT_scale=xs[:, c0 : c0 + P],
                rhs=wc[o][:, cols].bitcast(FP8X4),
                rhs_scale=wsc[o][:, cols],
                start=True,
                stop=True,
            )
            pss[(t, o, hf)] = ps

        def s_p1(t, o, hf):
            if (o, hf) == (0, 0):
                abs_[t] = abp.tile([P, 2, N], F32, tag="ab", name="ab")
                if t in gsize:
                    sts[t] = {
                        "sv": stp.tile([P, 2, 8], F32, tag="sv", name="sv"),
                        "ss": stp.tile([P, 8], F32, tag="ss", name="ss"),
                    }
            i = (t - gstart[t]) * 2 + o
            nc.vector.scalar_tensor_tensor(
                out=abs_[t][:, o, hf * 512 : (hf + 1) * 512],
                in0=pss[(t, o, hf)][:],
                scalar=-1.0,
                in1=bias[:, o * N + hf * 512 : o * N + (hf + 1) * 512],
                op0=ALU.mult,
                op1=ALU.subtract,
                accum_out=sts[gstart[t]]["sv"][:, hf, i : i + 1],
            )

        def s_sq(t, o):
            i = (t - gstart[t]) * 2 + o
            junk = jp.tile([P, N], BF16, tag="junk", name="junk")
            nc.scalar.activation(
                out=junk[:],
                in_=abs_[t][:, o, :],
                func=ACT.Square,
                bias=sts[gstart[t]]["sv"][:, 0, i : i + 1],
                scale=-512.0,
                accum_out=sts[gstart[t]]["ss"][:, i : i + 1],
            )

        def small(name, width):
            t_ = stp.tile([P, 8], F32, tag=name, name=name)
            return t_[:, 0:width]

        def s_ch(t0):
            g = gsize[t0]
            st = sts[t0]
            s0 = st["sv"][:, 0, 0 : 2 * g]
            s1 = st["sv"][:, 1, 0 : 2 * g]
            tt = nc.gpsimd.tensor_tensor
            dd = small("dd", 2 * g)
            tt(out=dd[:, :], in0=s1, in1=s0, op=ALU.subtract)
            d2 = small("d2", 2 * g)
            tt(out=d2[:, :], in0=dd[:, :], in1=dd[:, :], op=ALU.mult)
            sm = small("sm", 2 * g)
            tt(out=sm[:, :], in0=s0, in1=s1, op=ALU.add)
            qq = small("qq", 2 * g)
            nc.gpsimd.tensor_scalar(
                out=qq[:, :], in0=st["ss"][:, 0 : 2 * g], scalar1=1.0 / 256.0, scalar2=EPS * N * N, op0=ALU.mult, op1=ALU.add
            )
            vn = small("vn", 2 * g)
            tt(out=vn[:, :], in0=qq[:, :], in1=d2[:, :], op=ALU.subtract)
            rsn = small("rsn", 2 * g)
            for c0 in range(0, 2 * g, POWW):
                c1 = min(c0 + POWW, 2 * g)
                tt(out=rsn[:, c0:c1], in0=vn[:, c0:c1], in1=mhalf[:, 0 : c1 - c0], op=ALU.pow)
            vn_v = vn[:, :].rearrange("p (t o) -> p t o", o=2)
            rsn_v = rsn[:, :].rearrange("p (t o) -> p t o", o=2)
            sdn = small("sdn", g)
            tt(out=sdn[:, :], in0=vn_v[:, :, 1], in1=rsn_v[:, :, 1], op=ALU.mult)
            rho = small("rho", g)
            tt(out=rho[:, :], in0=sdn[:, :], in1=rsn_v[:, :, 0], op=ALU.mult)
            mm_ = small("mm_", 2 * g)
            tt(out=mm_[:, :], in0=sm[:, :], in1=rsn[:, :], op=ALU.mult)
            mm_v = mm_[:, :].rearrange("p (t o) -> p t o", o=2)
            c = small("c", g)
            tt(out=c[:, :], in0=mm_v[:, :, 0], in1=mm_v[:, :, 1], op=ALU.add)
            nsc = small("nsc", g)
            nc.gpsimd.tensor_scalar(
                out=nsc[:, :], in0=rsn_v[:, :, 1], scalar1=-1.0 * N, scalar2=0.0, op0=ALU.mult, op1=ALU.add
            )
            st["rho"] = rho
            st["c"] = c
            st["nsc"] = nsc

        def s_chv(t0):
            g = gsize[t0]
            w = 2 * g
            st = sts[t0]
            s0 = st["sv"][:, 0, 0:w]
            s1 = st["sv"][:, 1, 0:w]
            tt = nc.vector.tensor_tensor
            stt = nc.vector.scalar_tensor_tensor
            dd = small("dd", w)
            tt(out=dd[:, :], in0=s1, in1=s0, op=ALU.subtract)
            sm = small("sm", w)
            tt(out=sm[:, :], in0=s0, in1=s1, op=ALU.add)
            d2 = small("d2", w)
            tt(out=d2[:, :], in0=dd[:, :], in1=dd[:, :], op=ALU.mult)
            qq = small("qq", w)
            nc.vector.tensor_scalar(
                out=qq[:, :], in0=st["ss"][:, 0:w], scalar1=1.0 / 256.0, scalar2=EPS * N * N, op0=ALU.mult, op1=ALU.add
            )
            vn = small("vn", w)
            tt(out=vn[:, :], in0=qq[:, :], in1=d2[:, :], op=ALU.subtract)
            y0 = stp.tile([P, 8], I32, tag="y0", name="y0")
            nc.vector.tensor_scalar(
                out=y0[:, 0:w], in0=vn.bitcast(I32), scalar1=-0.5, scalar2=RSQRT_BITS, op0=ALU.mult, op1=ALU.add
            )
            y = y0[:, 0:w].bitcast(F32)
            for k in range(3):
                ny2 = small("ny2", w)
                stt(out=ny2[:, :], in0=y, scalar=-0.5, in1=y, op0=ALU.mult, op1=ALU.mult)
                vy = small("vy", w)
                tt(out=vy[:, :], in0=ny2[:, :], in1=vn[:, :], op=ALU.mult)
                yn = small("yn%d" % k, w)
                stt(out=yn[:, :], in0=vy[:, :], scalar=1.5, in1=y, op0=ALU.add, op1=ALU.mult)
                y = yn[:, :]
            y_v = y.rearrange("p (t o) -> p t o", o=2)
            vn_v = vn[:, :].rearrange("p (t o) -> p t o", o=2)
            sdn = small("sdn", g)
            tt(out=sdn[:, :], in0=vn_v[:, :, 1], in1=y_v[:, :, 1], op=ALU.mult)
            mm_ = small("mm_", w)
            tt(out=mm_[:, :], in0=sm[:, :], in1=y, op=ALU.mult)
            mm_v = mm_[:, :].rearrange("p (t o) -> p t o", o=2)
            nsc = small("nsc", g)
            nc.vector.tensor_scalar(out=nsc[:, :], in0=y_v[:, :, 1], scalar1=-1.0 * N, scalar2=0.0, op0=ALU.mult, op1=ALU.add)
            rho = small("rho", g)
            tt(out=rho[:, :], in0=sdn[:, :], in1=y_v[:, :, 0], op=ALU.mult)
            c = small("c", g)
            tt(out=c[:, :], in0=mm_v[:, :, 0], in1=mm_v[:, :, 1], op=ALU.add)
            st["rho"] = rho
            st["c"] = c
            st["nsc"] = nsc

        def s_diag(t):
            dg = dgp.tile([P, P], F32, tag="dg", name="dg")
            nc.gpsimd.tensor_scalar(
                out=dg[:], in0=ident[:], scalar1=sts[gstart[t]]["rho"][:, t - gstart[t] : t - gstart[t] + 1], scalar2=0.0, op0=ALU.mult, op1=ALU.add
            )
            dgs[t] = dg

        def s_join_pe(t, hf):
            ab = abs_[t]
            cols = slice(hf * 512, (hf + 1) * 512)
            ps = bank()
            nc.tensor.matmul(out=ps[:], lhsT=dgs[t][:], rhs=ab[:, 0, cols], start=True, stop=False)
            nc.tensor.matmul(out=ps[:], lhsT=ident[:], rhs=ab[:, 1, cols], start=False, stop=True)
            pss[("j", t, hf)] = ps

        def s_join_v(t):
            ab = abs_[t]
            rho = sts[gstart[t]]["rho"][:, t - gstart[t] : t - gstart[t] + 1]
            nc.vector.scalar_tensor_tensor(
                out=ab[:, 1, :], in0=ab[:, 0, :], scalar=rho, in1=ab[:, 1, :], op0=ALU.mult, op1=ALU.add
            )

        def s_sig(t):
            ot = op.tile([P, N], F32, tag="ot", name="ot")
            w = LW if t == NT - 1 else N
            c_ = sts[gstart[t]]["c"][:, t - gstart[t] : t - gstart[t] + 1]
            nsc_ = sts[gstart[t]]["nsc"][:, t - gstart[t] : t - gstart[t] + 1]
            if kind(t) == "P":
                for hf in range(2):
                    nc.scalar.activation(
                        out=ot[:, hf * 512 : (hf + 1) * 512], in_=pss[("j", t, hf)][:], func=ACT.Sigmoid, bias=c_, scale=nsc_
                    )
            else:
                for c0 in range(0, N, w):
                    nc.scalar.activation(
                        out=ot[:, c0 : c0 + w], in_=abs_[t][:, 1, c0 : c0 + w], func=ACT.Sigmoid, bias=c_, scale=nsc_
                    )
            for c0 in range(0, N, w):
                nc.sync.dma_start(out=out.rearrange("(p t) j -> p t j", t=NT)[:, t, c0 : c0 + w], in_=ot[:, c0 : c0 + w])

        heads = {}

        def h_tr(o, pr):
            tp = bank()
            for a in range(2):
                w_ = act_words(o, 2 * pr + a)
                for u in range(2):
                    q = 2 * a + u
                    nc.tensor.transpose(tp[:, q * P : (q + 1) * P], w_[:, u:256:2], ident[:])
            heads[(o, pr)] = tp

        def h_ev(o, pr):
            xg = xgp.tile([P, 1024], BF16, tag="xg", name="xg", align_bytes=64)
            dst = xg[:].bitcast(F32).rearrange("p (a r u) -> p a r u", a=2, u=2)
            nc.scalar.copy(out=dst, in_=heads[(o, pr)][:].rearrange("p (a u r) -> p a r u", a=2, u=2))
            heads[(o, pr)] = xg

        def h_q(o, pr):
            xc = const.tile([P, 256], U32, name="hxc%d%d" % (o, pr), align_bytes=64)
            xs = const.tile([P, 256], U8, name="hxs%d%d" % (o, pr), align_bytes=64)
            nc.vector.quantize_mx(out=xc[:].bitcast(FP8X4), scales=xs[:], in_=heads[(o, pr)][:])
            xcs[("head", o, pr)] = (xc, xs)

        def act_ready(ts):
            for t in ts:
                s_tr(t)
            for t in ts:
                s_ev(t)

        def mxs(ts, o, hf):
            for t in ts:
                s_mx(t, o, hf)

        def p1s(ts, o, hf):
            for t in ts:
                s_p1(t, o, hf)

        def sqs(ts, o):
            for t in ts:
                s_sq(t, o)

        def keep_warm(n):
            ps = bank()
            for k in range(n):
                nc.tensor.matmul(out=ps[:], lhsT=ones[:], rhs=idle[:], start=True, stop=True)

        first, second, four = (0, 1), (2, 3), (0, 1, 2, 3)
        if WARM[0]:
            keep_warm(WARM[0])
        w_transpose(0, 0, False)
        if WARM[1]:
            keep_warm(WARM[1])
        w_quantise(0, 0)
        h_tr(0, 0)
        h_ev(0, 0)
        h_q(0, 0)
        h_tr(0, 1)
        spread_bias(0)
        h_ev(0, 1)
        mxs(first, 0, 0)
        h_q(0, 1)
        p1s(first, 0, 0)
        w_transpose(0, 1, False)
        h_tr(1, 0)
        mxs(second, 0, 0)
        p1s(second, 0, 0)
        w_quantise(0, 1)
        h_ev(1, 0)
        h_tr(1, 1)
        h_ev(1, 1)
        w_transpose(1, 0, False)
        spread_bias(1)
        mxs(four, 0, 1)
        p1s(first, 0, 1)
        h_q(1, 0)
        w_quantise(1, 0)
        p1s(second, 0, 1)
        h_q(1, 1)
        sqs(first, 0)
        w_transpose(1, 1, False)
        mxs(four, 1, 0)
        p1s(first, 1, 0)
        w_quantise(1, 1)
        p1s(second, 1, 0)
        sqs(second, 0)
        act_ready((4, 5))
        mxs(four, 1, 1)
        s_q(4)
        p1s(first, 1, 1)
        if QB == 1:
            s_q(5)
        p1s(second, 1, 1)
        sqs(first, 1)
        act_ready((6,))
        sqs(second, 1)
        for t in range(7, EVL + 4):
            act_ready((t,))
        s_tr(EVL + 4)
        for o in range(2):
            for hf in range(2):
                s_mx(4, o, hf)

        def lag(t):
            return LAG

        def due(it, early=0):
            return [t for t in range(NT) if t + lag(t) - early == it]

        def chain_at(it):
            for t0 in gsize:
                if it == t0 + gsize[t0] - 1 + CHD + (VD if t0 >= VCH else 0):
                    if t0 >= VCH:
                        s_chv(t0)
                    else:
                        s_ch(t0)
                    for t in range(t0, t0 + gsize[t0]):
                        if kind(t) == "P":
                            s_diag(t)

        for it in range(HEAD):
            chain_at(it)

        def joins(it, pos):
            for (hf, early, pos_) in PJS:
                if pos == pos_:
                    for t in due(it, early):
                        if kind(t) == "P":
                            s_join_pe(t, hf)

        def ev_on_vector(t):
            return t >= EVMIN and EVV[t % len(EVV)] == "V"

        for it in range(HEAD, NT + LAG):
            chain_at(it)
            for k_ in VORD:
                if k_ == "q" and ok(it + QL):
                    s_q(it + QL)
                if k_ in "ab" and ok(it):
                    for hf in range(2):
                        s_p1(it, "ab".index(k_), hf)
                if k_ == "j":
                    for t in due(it):
                        if kind(t) == "V":
                            s_join_v(t)
                if k_ == "e" and ok(it + EVL) and ev_on_vector(it + EVL):
                    s_ev(it + EVL)
            for k_ in PORD:
                if k_ in "ab" and ok(it + 1):
                    for hf in range(2):
                        s_mx(it + 1, "ab".index(k_), hf)
                if k_ == "t" and ok(it + EVL + 1):
                    s_tr(it + EVL + 1)
                if k_ in "01":
                    for t in due(it, PJE[int(k_)]):
                        if kind(t) == "P":
                            s_join_pe(t, int(k_))
            for k_ in SORD:
                if k_ in "01" and ok(it):
                    s_sq(it, int(k_))
                if k_ == "s":
                    for t in due(it):
                        s_sig(t)
                if k_ == "e" and ok(it + EVL) and not ev_on_vector(it + EVL):
                    s_ev(it + EVL)
